import numpy as np
import ml_dtypes


def mxq(x, axis, fmt="e4m3"):
    dtype, down = {"e4m3": (ml_dtypes.float8_e4m3fn, 7), "e5m2": (ml_dtypes.float8_e5m2, 14)}[fmt]
    v = np.moveaxis(np.asarray(x, np.float32).astype(ml_dtypes.bfloat16).astype(np.float64), axis, -1)
    blocks = v.reshape(v.shape[:-1] + (-1, 32))
    amax = np.abs(blocks).max(-1, keepdims=True)
    byte = np.maximum(np.where(amax > 0, np.frexp(amax)[1] - 1 + 127, 0) - down, 1)
    scale = np.exp2(byte - 127.0)
    codes = (blocks / scale).astype(np.float32).astype(dtype).astype(np.float64)
    return np.moveaxis((codes * scale).reshape(v.shape), -1, axis)


WIDE = False


def mx_kscale(k):
    if not WIDE:
        return np.ones(k)
    levels = np.array([10, -10, 5, -5, 0])
    a = np.random.permutation(np.resize(levels, k // 512 * 4)).reshape(k // 512, 4)
    idx = np.arange(k)
    return np.exp2(a[idx // 512, idx % 128 // 32])


BF16 = ml_dtypes.bfloat16


def bf(x):
    return np.asarray(x, np.float32).astype(BF16)


def f64(x):
    return np.asarray(x).astype(np.float64)


B, S, D, DK, H = 8, 512, 512, 1024, 4
DH = D // H
LN_EPS = 1e-8


def split_heads(x):
    return x.reshape(B, S, H, DH).transpose(0, 2, 1, 3).reshape(B * H, S, DH)


def merge_heads(x):
    return x.reshape(B, H, S, DH).transpose(0, 2, 1, 3).reshape(B, S, D)


def setup_inputs():
    s = mx_kscale(DK)
    keep = np.random.random((B, S, 1)) > 0.25
    return {"q_relu": bf(np.maximum(np.random.standard_normal((B, S, D)) * 2.2, 0.0)),
            "k_relu": bf(np.maximum(np.random.standard_normal((B, S, D)) * 2.2, 0.0)),
            "keys": bf(np.random.standard_normal((B, S, DK)) * s),
            "Wv": bf(np.random.standard_normal((D, DK)) * 2.2 / np.sqrt(DK) / s[None, :]),
            "bv": bf(np.random.standard_normal(D) * 0.3),
            "queries": bf(np.random.standard_normal((B, S, D)) * keep),
            "ln_gamma": bf(1.0 + 0.1 * np.random.standard_normal(D)),
            "ln_beta": bf(0.1 * np.random.standard_normal(D))}


def reference(q_relu, k_relu, keys, Wv, bv, queries, ln_gamma, ln_beta):
    x = f64(queries)
    v = np.maximum((mxq(f64(keys), 2, "e4m3") @ mxq(f64(Wv), 1, "e4m3").T) + f64(bv), 0.0)
    q_, k_, v_ = split_heads(f64(q_relu)), split_heads(f64(k_relu)), split_heads(v)
    sc = q_ @ k_.transpose(0, 2, 1) / np.sqrt(DH)
    e = np.exp(sc - sc.max(-1, keepdims=True))
    mask = np.tile(np.where(np.abs(x).sum(-1, keepdims=True) > 0, 1.0, 0.0), (H, 1, 1))
    o = (mxq(e, 2, "e4m3") @ mxq(v_, 1, "e4m3")) / e.sum(-1, keepdims=True) * mask
    y = merge_heads(o) + x
    mu = y.mean(-1, keepdims=True)
    var = np.square(y - mu).mean(-1, keepdims=True)
    return (y - mu) / np.sqrt(var + LN_EPS) * f64(ln_gamma) + f64(ln_beta)

@@ -1,0 +1,317 @@
+from contextlib import ExitStack
+
+import concourse.mybir as mybir
+from concourse.masks import make_identity
+
+F32 = mybir.dt.float32
+BF16 = mybir.dt.bfloat16
+U32 = mybir.dt.uint32
+U8 = mybir.dt.uint8
+FP8X4 = mybir.dt.float8_e4m3fn_x4
+ALU = mybir.AluOpType
+ACT = mybir.ActivationFunctionType
+
+B, S, D, DK, H = 8, 512, 512, 1024, 4
+DH = D // H
+P = 128
+PACK = 4
+K_PASS = P * PACK
+PASSES = DK // K_PASS
+TILES = S // P
+PAIR = 2
+HALVES = TILES // PAIR
+SLOTS = HALVES * H
+SCALE = 1.0 / DH ** 0.5
+LN_EPS = 1e-8
+
+FLOPS = 2 * B * S * DK * D + 2 * 2 * B * H * S * S * DH
+
+
+def tile_multiheadattentionlayer_pa_t_kernel(
+    tc, q_relu, k_relu, keys, Wv, bv, queries, ln_gamma, ln_beta, out
+):
+    nc = tc.nc
+    with ExitStack() as ctx:
+        const = ctx.enter_context(tc.tile_pool(name="const", bufs=1))
+        loads = ctx.enter_context(tc.tile_pool(name="loads", bufs=2))
+        ready = ctx.enter_context(tc.tile_pool(name="ready", bufs=2))
+        flow = ctx.enter_context(tc.tile_pool(name="flow", bufs=3))
+        score_ps = ctx.enter_context(tc.psum_pool(name="score_ps", bufs=2))
+        et_ps = ctx.enter_context(tc.psum_pool(name="et_ps", bufs=2))
+        o_ps = ctx.enter_context(tc.psum_pool(name="o_ps", bufs=2))
+        prep_ps = ctx.enter_context(tc.psum_pool(name="prep_ps", bufs=2))
+
+        batch = {}
+
+        def load_batch(b):
+            keys_sb = loads.tile([P, TILES * DK], BF16, name="keys_sb")
+            nc.sync.dma_start(
+                out=keys_sb[:].rearrange("q (u x) -> q u x", u=2),
+                in_=keys[b].rearrange("(u q e) k -> q u (e k)", u=2, e=2),
+            )
+            q_sb = loads.tile([P, TILES, D], BF16, name="q_sb")
+            nc.sync.dma_start(out=q_sb[:], in_=q_relu[b].rearrange("(t p) d -> p t d", p=P))
+            k_sb = loads.tile([P, TILES, D], BF16, name="k_sb")
+            nc.sync.dma_start(out=k_sb[:], in_=k_relu[b].rearrange("(t p) d -> p t d", p=P))
+            batch[b] = {"keys_sb": keys_sb, "q_sb": q_sb, "k_sb": k_sb}
+
+        wv_sb = const.tile([P, TILES * DK], BF16, name="wv_sb")
+        nc.sync.dma_start(
+            out=wv_sb[:].rearrange("p (t k) -> p t k", t=TILES), in_=Wv.rearrange("(t p) k -> p t k", p=P)
+        )
+        load_batch(0)
+        bias_bc = const.tile([P, D], BF16, name="bias_bc")
+        nc.sync.dma_start(out=bias_bc[:], in_=bv.partition_broadcast(P))
+        x_sb = const.tile([P, B, TILES, D], BF16, name="x_sb")
+        for b in range(B // 2):
+            nc.sync.dma_start(out=x_sb[:, b], in_=queries[b].rearrange("(t p) d -> p t d", p=P))
+        gamma_raw = const.tile([P, D], BF16, name="gamma_raw")
+        nc.sync.dma_start(out=gamma_raw[:], in_=ln_gamma.partition_broadcast(P))
+        beta_raw = const.tile([P, D], BF16, name="beta_raw")
+        nc.sync.dma_start(out=beta_raw[:], in_=ln_beta.partition_broadcast(P))
+        load_batch(1)
+        for b in range(B // 2, B):
+            nc.sync.dma_start(out=x_sb[:, b], in_=queries[b].rearrange("(t p) d -> p t d", p=P))
+
+        ident_bf = const.tile([P, P], BF16, name="ident_bf")
+        make_identity(nc, ident_bf[:])
+        ident_f32 = const.tile([P, P], F32, name="ident_f32")
+        make_identity(nc, ident_f32[:])
+        neg_half = const.tile([P, PAIR], F32, name="neg_half")
+        nc.gpsimd.memset(neg_half[:], -0.5)
+        gamma_bc = const.tile([P, D], F32, name="gamma_bc")
+        nc.vector.tensor_copy(out=gamma_bc[:], in_=gamma_raw[:])
+        beta_bc = const.tile([P, D], F32, name="beta_bc")
+        nc.vector.tensor_copy(out=beta_bc[:], in_=beta_raw[:])
+        abs_sum = const.tile([P, B * TILES], F32, name="abs_sum")
+        mask01 = const.tile([P, B * TILES], F32, name="mask01")
+
+        def pairs_onto_partitions(rows_sb, grouped, g, pair):
+            words = rows_sb[:].bitcast(F32)
+            bank = prep_ps.tile([P, 2, PAIR * P], F32, name="words_t", tag="prep")
+            for u in range(2):
+                for r in range(PAIR):
+                    first = (PAIR * pair + r) * (DK // 2) + g * (K_PASS // 2) + u * P
+                    nc.tensor.transpose(bank[:, u, r * P : (r + 1) * P], words[:, first : first + P], ident_f32[:])
+            dst = grouped[:].rearrange("q (g s u) -> q g s u", g=PASSES, u=2)
+            rows = slice(pair * PAIR * P, (pair + 1) * PAIR * P)
+            nc.scalar.copy(out=dst[:, g, rows, :], in_=bank[:].rearrange("q u s -> q s u"))
+
+        def quantise_pass(grouped, codes, scales, g):
+            nc.vector.quantize_mx(
+                out=codes[:, g * S : (g + 1) * S].bitcast(FP8X4),
+                scales=scales[:, g * S : (g + 1) * S],
+                in_=grouped[:].bitcast(BF16)[:, g * S * PACK : (g + 1) * S * PACK],
+            )
+
+        def heads_onto_partitions(rows_sb, heads_t, head_pair):
+            bank = prep_ps.tile([P, PAIR, S], BF16, name="heads_bank", tag="prep")
+            for hh in range(PAIR):
+                h = PAIR * head_pair + hh
+                for t in range(TILES):
+                    nc.tensor.transpose(
+                        bank[:, hh, t * P : (t + 1) * P], rows_sb[:, t, h * DH : (h + 1) * DH], ident_bf[:]
+                    )
+            nc.scalar.copy(out=heads_t[:, PAIR * head_pair : PAIR * (head_pair + 1), :], in_=bank[:])
+
+        def project_values(tiles, h):
+            bank = prep_ps.tile([P, TILES, DH], F32, name="v_bank", tag="prep")
+            for t in range(TILES):
+                for g in range(PASSES):
+                    key_cols = slice(g * S + t * P, g * S + (t + 1) * P)
+                    out_cols = slice(g * D + h * DH, g * D + (h + 1) * DH)
+                    nc.tensor.matmul_mx(
+                        out=bank[:, t, :],
+                        lhsT=tiles["keys_codes"][:, key_cols].bitcast(FP8X4),
+                        lhsT_scale=tiles["keys_scales"][:, key_cols],
+                        rhs=wv_codes[:, out_cols].bitcast(FP8X4),
+                        rhs_scale=wv_scales[:, out_cols],
+                        start=(g == 0),
+                        stop=(g == PASSES - 1),
+                    )
+            nc.vector.tensor_tensor(
+                out=tiles["v_grouped"][:, h, :, :],
+                in0=bank[:].rearrange("q t c -> q c t"),
+                in1=bias_bc[:, h * DH : (h + 1) * DH].unsqueeze(2).to_broadcast([P, DH, TILES]),
+                op=ALU.add,
+            )
+
+        def prepare_slot(b, slot):
+            tiles = batch[b]
+            if slot == 0:
+                tiles["keys_grouped"] = ready.tile([P, PASSES * S * 2], F32, name="keys_grouped", align_bytes=64)
+            if slot == 1:
+                tiles["keys_codes"] = ready.tile([P, PASSES * S], U32, name="keys_codes", align_bytes=64)
+                tiles["keys_scales"] = ready.tile([P, PASSES * S], U8, name="keys_scales", align_bytes=64)
+            if slot == 2:
+                tiles["q_t"] = ready.tile([P, H, S], BF16, name="q_t")
+            if slot == 3:
+                tiles["v_grouped"] = ready.tile([P, H, DH, PACK], BF16, name="v_grouped", align_bytes=64)
+            if slot == 4:
+                tiles["k_t"] = ready.tile([P, H, S], BF16, name="k_t")
+            if slot < 2:
+                for pair in range(TILES // PAIR):
+                    pairs_onto_partitions(tiles["keys_sb"], tiles["keys_grouped"], slot, pair)
+            if 1 <= slot < 3:
+                quantise_pass(tiles["keys_grouped"], tiles["keys_codes"], tiles["keys_scales"], slot - 1)
+            if 2 <= slot < 4:
+                heads_onto_partitions(tiles["q_sb"], tiles["q_t"], slot - 2)
+            if 4 <= slot < 6:
+                heads_onto_partitions(tiles["k_sb"], tiles["k_t"], slot - 4)
+            if 3 <= slot < 7:
+                project_values(tiles, slot - 3)
+            if slot == 7:
+                v_flat = tiles["v_grouped"][:].rearrange("q h c t -> q (h c t)")
+                nc.vector.tensor_scalar_max(out=v_flat, in0=v_flat, scalar1=0.0)
+
+        def quantise_values(b):
+            tiles = batch[b]
+            tiles["v_codes"] = ready.tile([P, D], U32, name="v_codes", align_bytes=64)
+            tiles["v_scales"] = ready.tile([P, D], U8, name="v_scales", align_bytes=64)
+            nc.vector.quantize_mx(
+                out=tiles["v_codes"][:].bitcast(FP8X4),
+                scales=tiles["v_scales"][:],
+                in_=tiles["v_grouped"][:].rearrange("q h c t -> q (h c t)"),
+            )
+
+        def row_mask(b):
+            for t in range(TILES):
+                unread = flow.tile([P, D], BF16, name="unread")
+                nc.scalar.activation(
+                    out=unread[:], in_=x_sb[:, b, t, :], func=ACT.Abs, accum_out=abs_sum[:, b * TILES + t : b * TILES + t + 1]
+                )
+            cols = slice(b * TILES, (b + 1) * TILES)
+            nc.vector.tensor_single_scalar(out=mask01[:, cols], in_=abs_sum[:, cols], scalar=0.0, op=ALU.is_gt)
+
+        wv_grouped = const.tile([P, PASSES * D * 2], F32, name="wv_grouped", align_bytes=64)
+        wv_codes = const.tile([P, PASSES * D], U32, name="wv_codes", align_bytes=64)
+        wv_scales = const.tile([P, PASSES * D], U8, name="wv_scales", align_bytes=64)
+        for g in range(PASSES):
+            for pair in range(TILES // PAIR):
+                pairs_onto_partitions(wv_sb, wv_grouped, g, pair)
+        for g in range(PASSES):
+            quantise_pass(wv_grouped, wv_codes, wv_scales, g)
+        for slot in range(SLOTS):
+            prepare_slot(0, slot)
+
+        steps = [(b, a, h) for b in range(B) for a in range(HALVES) for h in range(H)]
+        live = {}
+        y_of = {}
+
+        def scores_and_row_max(j):
+            b, a, h = steps[j]
+            neg_max = flow.tile([P, PAIR], F32, name="neg_max")
+            neg_s = []
+            for i in range(PAIR):
+                t = PAIR * a + i
+                bank = score_ps.tile([P, S], F32, name="score_bank")
+                nc.tensor.matmul(
+                    out=bank[:], lhsT=batch[b]["q_t"][:, h, t * P : (t + 1) * P], rhs=batch[b]["k_t"][:, h, :],
+                    start=True, stop=True,
+                )
+                neg_s.append(flow.tile([P, S], F32, name="neg_s", bufs=6))
+                nc.vector.tensor_scalar(
+                    out=neg_s[i][:], in0=bank[:], scalar1=-SCALE, scalar2=None, op0=ALU.mult, op1=ALU.min,
+                    accum_out=neg_max[:, i : i + 1],
+                )
+            live[j] = {"neg_s": neg_s, "neg_max": neg_max}
+
+        def exponentials(j):
+            tiles = live[j]
+            tiles["e_sb"] = flow.tile([P, PAIR * S], BF16, name="e_sb")
+            tiles["row_sum"] = flow.tile([P, PAIR], F32, name="row_sum")
+            for i in range(PAIR):
+                nc.scalar.activation(
+                    out=tiles["e_sb"][:, i * S : (i + 1) * S], in_=tiles["neg_s"][i][:], func=ACT.Exp,
+                    scale=-1.0, bias=tiles["neg_max"][:, i : i + 1], accum_out=tiles["row_sum"][:, i : i + 1],
+                )
+
+        def keys_of_e_onto_partitions(j):
+            tiles = live[j]
+            words = tiles["e_sb"][:].bitcast(F32)
+            bank = et_ps.tile([P, PAIR, 2, P], F32, name="et_bank")
+            for i in range(PAIR):
+                for u in range(2):
+                    first = i * (S // 2) + u * P
+                    nc.tensor.transpose(bank[:, i, u, :], words[:, first : first + P], ident_f32[:])
+            tiles["e_grouped"] = flow.tile([P, PAIR * P * 2], F32, name="e_grouped", align_bytes=64)
+            nc.scalar.copy(
+                out=tiles["e_grouped"][:].rearrange("q (i r u) -> q i r u", i=PAIR, u=2),
+                in_=bank[:].rearrange("q i u r -> q i r u"),
+            )
+
+        def attend(j):
+            b, a, h = steps[j]
+            tiles = live[j]
+            e_codes = flow.tile([P, PAIR * P], U32, name="e_codes", align_bytes=64)
+            e_scales = flow.tile([P, PAIR * P], U8, name="e_scales", align_bytes=64)
+            nc.vector.quantize_mx(out=e_codes[:].bitcast(FP8X4), scales=e_scales[:], in_=tiles["e_grouped"][:].bitcast(BF16))
+            bank = o_ps.tile([P, PAIR, DH], F32, name="o_bank")
+            for i in range(PAIR):
+                nc.tensor.matmul_mx(
+                    out=bank[:, i, :],
+                    lhsT=e_codes[:, i * P : (i + 1) * P].bitcast(FP8X4),
+                    lhsT_scale=e_scales[:, i * P : (i + 1) * P],
+                    rhs=batch[b]["v_codes"][:, h * DH : (h + 1) * DH].bitcast(FP8X4),
+                    rhs_scale=batch[b]["v_scales"][:, h * DH : (h + 1) * DH],
+                    start=True,
+                    stop=True,
+                )
+            mask_first = ((H * b + h) % B) * TILES + PAIR * a
+            inv_sum = flow.tile([P, PAIR], F32, name="inv_sum")
+            nc.vector.reciprocal(out=inv_sum[:], in_=tiles["row_sum"][:])
+            row_scale = flow.tile([P, PAIR], F32, name="row_scale")
+            nc.vector.tensor_tensor(out=row_scale[:], in0=inv_sum[:], in1=mask01[:, mask_first : mask_first + PAIR], op=ALU.mult)
+            if h == 0:
+                y_of[(b, a)] = flow.tile([P, PAIR, D], F32, name="y")
+            y = y_of[(b, a)]
+            for i in range(PAIR):
+                nc.vector.scalar_tensor_tensor(
+                    out=y[:, i, h * DH : (h + 1) * DH], in0=bank[:, i, :], scalar=row_scale[:, i : i + 1],
+                    in1=x_sb[:, b, PAIR * a + i, h * DH : (h + 1) * DH], op0=ALU.mult, op1=ALU.add,
+                )
+            if h == H - 1:
+                layer_norm_and_store(b, a, y)
+
+        def layer_norm_and_store(b, a, y):
+            stats = flow.tile([P, PAIR, 6], F32, name="stats")
+            mean_var = flow.tile([P, PAIR, 2], F32, name="mean_var")
+            for i in range(PAIR):
+                nc.vector.bn_stats(out=stats[:, i, :], in_=y[:, i, :])
+            for i in range(PAIR):
+                nc.vector.bn_aggr(out=mean_var[:, i, :], in_=stats[:, i, :])
+            var_eps = flow.tile([P, PAIR], F32, name="var_eps")
+            nc.gpsimd.tensor_scalar(out=var_eps[:], in0=mean_var[:, :, 1], scalar1=LN_EPS, scalar2=1.0, op0=ALU.add, op1=ALU.mult)
+            neg_mean = flow.tile([P, PAIR], F32, name="neg_mean")
+            nc.gpsimd.tensor_scalar(out=neg_mean[:], in0=mean_var[:, :, 0], scalar1=-1.0, scalar2=0.0, op0=ALU.mult, op1=ALU.add)
+            inv_std = flow.tile([P, PAIR], F32, name="inv_std")
+            nc.gpsimd.tensor_tensor(out=inv_std[:], in0=var_eps[:], in1=neg_half[:], op=ALU.pow)
+            for i in range(PAIR):
+                nc.gpsimd.tensor_scalar(
+                    out=y[:, i, :], in0=y[:, i, :], scalar1=neg_mean[:, i : i + 1], scalar2=inv_std[:, i : i + 1],
+                    op0=ALU.add, op1=ALU.mult,
+                )
+            nc.gpsimd.tensor_tensor(out=y[:], in0=y[:], in1=gamma_bc[:].unsqueeze(1).to_broadcast([P, PAIR, D]), op=ALU.mult)
+            nc.gpsimd.tensor_tensor(out=y[:], in0=y[:], in1=beta_bc[:].unsqueeze(1).to_broadcast([P, PAIR, D]), op=ALU.add)
+            rows = slice(a * PAIR * P, (a + 1) * PAIR * P)
+            nc.sync.dma_start(out=out[b, rows, :].rearrange("(t p) d -> p t d", p=P), in_=y[:])
+
+        for j in range(len(steps) + 2):
+            if j < len(steps):
+                b, a, h = steps[j]
+                slot = H * a + h
+                if slot == 0:
+                    quantise_values(b)
+                    if b + 2 < B:
+                        load_batch(b + 2)
+                scores_and_row_max(j)
+            if 1 <= j <= len(steps):
+                exponentials(j - 1)
+            if j < B:
+                row_mask(j)
+            if j < len(steps) and b + 1 < B:
+                prepare_slot(b + 1, slot)
+            if 1 <= j <= len(steps):
+                keys_of_e_onto_partitions(j - 1)
+            if j >= 2:
+                attend(j - 2)

@@ -23,6 +23,7 @@ HALVES = TILES // PAIR
 SLOTS = HALVES * H
 SCALE = 1.0 / DH ** 0.5
 LN_EPS = 1e-8
+LN_PIECE = 256
 
 FLOPS = 2 * B * S * DK * D + 2 * 2 * B * H * S * S * DH
 
@@ -291,8 +292,11 @@ def tile_multiheadattentionlayer_pa_t_kernel(
                     out=y[:, i, :], in0=y[:, i, :], scalar1=neg_mean[:, i : i + 1], scalar2=inv_std[:, i : i + 1],
                     op0=ALU.add, op1=ALU.mult,
                 )
-            nc.gpsimd.tensor_tensor(out=y[:], in0=y[:], in1=gamma_bc[:].unsqueeze(1).to_broadcast([P, PAIR, D]), op=ALU.mult)
-            nc.gpsimd.tensor_tensor(out=y[:], in0=y[:], in1=beta_bc[:].unsqueeze(1).to_broadcast([P, PAIR, D]), op=ALU.add)
+            pieces = [(i, slice(first, first + LN_PIECE)) for i in range(PAIR) for first in range(0, D, LN_PIECE)]
+            for i, cols in pieces:
+                nc.gpsimd.tensor_tensor(out=y[:, i, cols], in0=y[:, i, cols], in1=gamma_bc[:, cols], op=ALU.mult)
+            for i, cols in pieces:
+                nc.gpsimd.tensor_tensor(out=y[:, i, cols], in0=y[:, i, cols], in1=beta_bc[:, cols], op=ALU.add)
             rows = slice(a * PAIR * P, (a + 1) * PAIR * P)
             nc.sync.dma_start(out=out[b, rows, :].rearrange("(t p) d -> p t d", p=P), in_=y[:])
 

@@ -24,6 +24,9 @@ SLOTS = HALVES * H
 SCALE = 1.0 / DH ** 0.5
 LN_EPS = 1e-8
 LN_PIECE = 256
+EXP_LAG = 1
+ATTEND_LAG = 2
+STATS_LAG = 3
 
 FLOPS = 2 * B * S * DK * D + 2 * 2 * B * H * S * S * DH
 
@@ -64,15 +67,13 @@ def tile_multiheadattentionlayer_pa_t_kernel(
         bias_bc = const.tile([P, D], BF16, name="bias_bc")
         nc.sync.dma_start(out=bias_bc[:], in_=bv.partition_broadcast(P))
         x_sb = const.tile([P, B, TILES, D], BF16, name="x_sb")
-        for b in range(B // 2):
+        for b in range(B):
             nc.sync.dma_start(out=x_sb[:, b], in_=queries[b].rearrange("(t p) d -> p t d", p=P))
         gamma_raw = const.tile([P, D], BF16, name="gamma_raw")
         nc.sync.dma_start(out=gamma_raw[:], in_=ln_gamma.partition_broadcast(P))
         beta_raw = const.tile([P, D], BF16, name="beta_raw")
         nc.sync.dma_start(out=beta_raw[:], in_=ln_beta.partition_broadcast(P))
         load_batch(1)
-        for b in range(B // 2, B):
-            nc.sync.dma_start(out=x_sb[:, b], in_=queries[b].rearrange("(t p) d -> p t d", p=P))
 
         ident_bf = const.tile([P, P], BF16, name="ident_bf")
         make_identity(nc, ident_bf[:])
@@ -84,8 +85,6 @@ def tile_multiheadattentionlayer_pa_t_kernel(
         nc.vector.tensor_copy(out=gamma_bc[:], in_=gamma_raw[:])
         beta_bc = const.tile([P, D], F32, name="beta_bc")
         nc.vector.tensor_copy(out=beta_bc[:], in_=beta_raw[:])
-        abs_sum = const.tile([P, B * TILES], F32, name="abs_sum")
-        mask01 = const.tile([P, B * TILES], F32, name="mask01")
 
         def pairs_onto_partitions(rows_sb, grouped, g, pair):
             words = rows_sb[:].bitcast(F32)
@@ -130,37 +129,45 @@ def tile_multiheadattentionlayer_pa_t_kernel(
                         start=(g == 0),
                         stop=(g == PASSES - 1),
                     )
+            tiles["v_bank"] = bank
+
+        def add_bias(tiles, h):
             nc.vector.tensor_tensor(
                 out=tiles["v_grouped"][:, h, :, :],
-                in0=bank[:].rearrange("q t c -> q c t"),
+                in0=tiles["v_bank"][:].rearrange("q t c -> q c t"),
                 in1=bias_bc[:, h * DH : (h + 1) * DH].unsqueeze(2).to_broadcast([P, DH, TILES]),
                 op=ALU.add,
             )
 
-        def prepare_slot(b, slot):
+        def prepare_on_tensor(b, slot):
             tiles = batch[b]
+            if 3 <= slot < 7:
+                project_values(tiles, slot - 3)
             if slot == 0:
                 tiles["keys_grouped"] = ready.tile([P, PASSES * S * 2], F32, name="keys_grouped", align_bytes=64)
-            if slot == 1:
-                tiles["keys_codes"] = ready.tile([P, PASSES * S], U32, name="keys_codes", align_bytes=64)
-                tiles["keys_scales"] = ready.tile([P, PASSES * S], U8, name="keys_scales", align_bytes=64)
-            if slot == 2:
-                tiles["q_t"] = ready.tile([P, H, S], BF16, name="q_t")
-            if slot == 3:
-                tiles["v_grouped"] = ready.tile([P, H, DH, PACK], BF16, name="v_grouped", align_bytes=64)
-            if slot == 4:
-                tiles["k_t"] = ready.tile([P, H, S], BF16, name="k_t")
             if slot < 2:
                 for pair in range(TILES // PAIR):
                     pairs_onto_partitions(tiles["keys_sb"], tiles["keys_grouped"], slot, pair)
-            if 1 <= slot < 3:
-                quantise_pass(tiles["keys_grouped"], tiles["keys_codes"], tiles["keys_scales"], slot - 1)
+            if slot == 2:
+                tiles["q_t"] = ready.tile([P, H, S], BF16, name="q_t")
             if 2 <= slot < 4:
                 heads_onto_partitions(tiles["q_sb"], tiles["q_t"], slot - 2)
+            if slot == 4:
+                tiles["k_t"] = ready.tile([P, H, S], BF16, name="k_t")
             if 4 <= slot < 6:
                 heads_onto_partitions(tiles["k_sb"], tiles["k_t"], slot - 4)
+
+        def prepare_on_vector(b, slot):
+            tiles = batch[b]
+            if slot == 1:
+                tiles["keys_codes"] = ready.tile([P, PASSES * S], U32, name="keys_codes", align_bytes=64)
+                tiles["keys_scales"] = ready.tile([P, PASSES * S], U8, name="keys_scales", align_bytes=64)
+            if 1 <= slot < 3:
+                quantise_pass(tiles["keys_grouped"], tiles["keys_codes"], tiles["keys_scales"], slot - 1)
+            if slot == 3:
+                tiles["v_grouped"] = ready.tile([P, H, DH, PACK], BF16, name="v_grouped", align_bytes=64)
             if 3 <= slot < 7:
-                project_values(tiles, slot - 3)
+                add_bias(tiles, slot - 3)
             if slot == 7:
                 v_flat = tiles["v_grouped"][:].rearrange("q h c t -> q (h c t)")
                 nc.vector.tensor_scalar_max(out=v_flat, in0=v_flat, scalar1=0.0)
@@ -175,15 +182,6 @@ def tile_multiheadattentionlayer_pa_t_kernel(
                 in_=tiles["v_grouped"][:].rearrange("q h c t -> q (h c t)"),
             )
 
-        def row_mask(b):
-            for t in range(TILES):
-                unread = flow.tile([P, D], BF16, name="unread")
-                nc.scalar.activation(
-                    out=unread[:], in_=x_sb[:, b, t, :], func=ACT.Abs, accum_out=abs_sum[:, b * TILES + t : b * TILES + t + 1]
-                )
-            cols = slice(b * TILES, (b + 1) * TILES)
-            nc.vector.tensor_single_scalar(out=mask01[:, cols], in_=abs_sum[:, cols], scalar=0.0, op=ALU.is_gt)
-
         wv_grouped = const.tile([P, PASSES * D * 2], F32, name="wv_grouped", align_bytes=64)
         wv_codes = const.tile([P, PASSES * D], U32, name="wv_codes", align_bytes=64)
         wv_scales = const.tile([P, PASSES * D], U8, name="wv_scales", align_bytes=64)
@@ -193,29 +191,52 @@ def tile_multiheadattentionlayer_pa_t_kernel(
         for g in range(PASSES):
             quantise_pass(wv_grouped, wv_codes, wv_scales, g)
         for slot in range(SLOTS):
-            prepare_slot(0, slot)
+            prepare_on_tensor(0, slot)
+            prepare_on_vector(0, slot)
+
+        abs_sum = const.tile([P, B * TILES], F32, name="abs_sum")
+        mask01 = const.tile([P, B * TILES], F32, name="mask01")
+        for b in range(B):
+            cols = slice(b * TILES, (b + 1) * TILES)
+            if b % 2 == 0:
+                for t in range(TILES):
+                    unread = flow.tile([P, D], BF16, name="unread")
+                    nc.scalar.activation(
+                        out=unread[:], in_=x_sb[:, b, t, :], func=ACT.Abs,
+                        accum_out=abs_sum[:, b * TILES + t : b * TILES + t + 1],
+                    )
+                nc.vector.tensor_single_scalar(out=mask01[:, cols], in_=abs_sum[:, cols], scalar=0.0, op=ALU.is_gt)
+            else:
+                for t in range(TILES):
+                    unread = flow.tile([P, D], BF16, name="unread_v")
+                    nc.vector.tensor_scalar(
+                        out=unread[:], in0=x_sb[:, b, t, :], scalar1=0.0, scalar2=None, op0=ALU.not_equal, op1=ALU.max,
+                        accum_out=mask01[:, b * TILES + t : b * TILES + t + 1],
+                    )
 
         steps = [(b, a, h) for b in range(B) for a in range(HALVES) for h in range(H)]
         live = {}
         y_of = {}
 
-        def scores_and_row_max(j):
+        def scores(j, i):
             b, a, h = steps[j]
-            neg_max = flow.tile([P, PAIR], F32, name="neg_max")
-            neg_s = []
-            for i in range(PAIR):
-                t = PAIR * a + i
-                bank = score_ps.tile([P, S], F32, name="score_bank")
-                nc.tensor.matmul(
-                    out=bank[:], lhsT=batch[b]["q_t"][:, h, t * P : (t + 1) * P], rhs=batch[b]["k_t"][:, h, :],
-                    start=True, stop=True,
-                )
-                neg_s.append(flow.tile([P, S], F32, name="neg_s", bufs=6))
-                nc.vector.tensor_scalar(
-                    out=neg_s[i][:], in0=bank[:], scalar1=-SCALE, scalar2=None, op0=ALU.mult, op1=ALU.min,
-                    accum_out=neg_max[:, i : i + 1],
-                )
-            live[j] = {"neg_s": neg_s, "neg_max": neg_max}
+            t = PAIR * a + i
+            bank = score_ps.tile([P, S], F32, name="score_bank")
+            nc.tensor.matmul(
+                out=bank[:], lhsT=batch[b]["q_t"][:, h, t * P : (t + 1) * P], rhs=batch[b]["k_t"][:, h, :],
+                start=True, stop=True,
+            )
+            if i == 0:
+                live[j] = {"neg_max": flow.tile([P, PAIR], F32, name="neg_max")}
+            live[j]["score_bank", i] = bank
+
+        def row_max(j, i):
+            tiles = live[j]
+            tiles["neg_s", i] = flow.tile([P, S], F32, name="neg_s", bufs=6)
+            nc.vector.tensor_scalar(
+                out=tiles["neg_s", i][:], in0=tiles["score_bank", i][:], scalar1=-SCALE, scalar2=None,
+                op0=ALU.mult, op1=ALU.min, accum_out=tiles["neg_max"][:, i : i + 1],
+            )
 
         def exponentials(j):
             tiles = live[j]
@@ -223,7 +244,7 @@ def tile_multiheadattentionlayer_pa_t_kernel(
             tiles["row_sum"] = flow.tile([P, PAIR], F32, name="row_sum")
             for i in range(PAIR):
                 nc.scalar.activation(
-                    out=tiles["e_sb"][:, i * S : (i + 1) * S], in_=tiles["neg_s"][i][:], func=ACT.Exp,
+                    out=tiles["e_sb"][:, i * S : (i + 1) * S], in_=tiles["neg_s", i][:], func=ACT.Exp,
                     scale=-1.0, bias=tiles["neg_max"][:, i : i + 1], accum_out=tiles["row_sum"][:, i : i + 1],
                 )
 
@@ -241,7 +262,21 @@ def tile_multiheadattentionlayer_pa_t_kernel(
                 in_=bank[:].rearrange("q i u r -> q i r u"),
             )
 
-        def attend(j):
+        def invert_row_sums(j):
+            tiles = live[j]
+            tiles["inv_sum"] = flow.tile([P, PAIR], F32, name="inv_sum")
+            nc.vector.reciprocal(out=tiles["inv_sum"][:], in_=tiles["row_sum"][:])
+
+        def apply_mask(j):
+            b, a, h = steps[j]
+            tiles = live[j]
+            first = ((H * b + h) % B) * TILES + PAIR * a
+            tiles["row_scale"] = flow.tile([P, PAIR], F32, name="row_scale")
+            nc.vector.tensor_tensor(
+                out=tiles["row_scale"][:], in0=tiles["inv_sum"][:], in1=mask01[:, first : first + PAIR], op=ALU.mult
+            )
+
+        def e_times_v(j):
             b, a, h = steps[j]
             tiles = live[j]
             e_codes = flow.tile([P, PAIR * P], U32, name="e_codes", align_bytes=64)
@@ -258,41 +293,40 @@ def tile_multiheadattentionlayer_pa_t_kernel(
                     start=True,
                     stop=True,
                 )
-            mask_first = ((H * b + h) % B) * TILES + PAIR * a
-            inv_sum = flow.tile([P, PAIR], F32, name="inv_sum")
-            nc.vector.reciprocal(out=inv_sum[:], in_=tiles["row_sum"][:])
-            row_scale = flow.tile([P, PAIR], F32, name="row_scale")
-            nc.vector.tensor_tensor(out=row_scale[:], in0=inv_sum[:], in1=mask01[:, mask_first : mask_first + PAIR], op=ALU.mult)
+            tiles["o_bank"] = bank
+
+        def add_residual(j):
+            b, a, h = steps[j]
+            tiles = live[j]
             if h == 0:
-                y_of[(b, a)] = flow.tile([P, PAIR, D], F32, name="y")
-            y = y_of[(b, a)]
+                y_of[b, a] = {
+                    "y": flow.tile([P, PAIR, D], F32, name="y"),
+                    "stats": flow.tile([P, PAIR, 6], F32, name="stats"),
+                }
             for i in range(PAIR):
                 nc.vector.scalar_tensor_tensor(
-                    out=y[:, i, h * DH : (h + 1) * DH], in0=bank[:, i, :], scalar=row_scale[:, i : i + 1],
-                    in1=x_sb[:, b, PAIR * a + i, h * DH : (h + 1) * DH], op0=ALU.mult, op1=ALU.add,
+                    out=y_of[b, a]["y"][:, i, h * DH : (h + 1) * DH], in0=tiles["o_bank"][:, i, :],
+                    scalar=tiles["row_scale"][:, i : i + 1], in1=x_sb[:, b, PAIR * a + i, h * DH : (h + 1) * DH],
+                    op0=ALU.mult, op1=ALU.add,
                 )
-            if h == H - 1:
-                layer_norm_and_store(b, a, y)
 
-        def layer_norm_and_store(b, a, y):
-            stats = flow.tile([P, PAIR, 6], F32, name="stats")
+        def layer_norm_and_store(b, a):
+            y = y_of[b, a]["y"]
             mean_var = flow.tile([P, PAIR, 2], F32, name="mean_var")
             for i in range(PAIR):
-                nc.vector.bn_stats(out=stats[:, i, :], in_=y[:, i, :])
-            for i in range(PAIR):
-                nc.vector.bn_aggr(out=mean_var[:, i, :], in_=stats[:, i, :])
+                nc.vector.bn_aggr(out=mean_var[:, i, :], in_=y_of[b, a]["stats"][:, i, :])
             var_eps = flow.tile([P, PAIR], F32, name="var_eps")
             nc.gpsimd.tensor_scalar(out=var_eps[:], in0=mean_var[:, :, 1], scalar1=LN_EPS, scalar2=1.0, op0=ALU.add, op1=ALU.mult)
             neg_mean = flow.tile([P, PAIR], F32, name="neg_mean")
             nc.gpsimd.tensor_scalar(out=neg_mean[:], in0=mean_var[:, :, 0], scalar1=-1.0, scalar2=0.0, op0=ALU.mult, op1=ALU.add)
             inv_std = flow.tile([P, PAIR], F32, name="inv_std")
             nc.gpsimd.tensor_tensor(out=inv_std[:], in0=var_eps[:], in1=neg_half[:], op=ALU.pow)
-            for i in range(PAIR):
+            pieces = [(i, slice(first, first + LN_PIECE)) for i in range(PAIR) for first in range(0, D, LN_PIECE)]
+            for i, cols in pieces:
                 nc.gpsimd.tensor_scalar(
-                    out=y[:, i, :], in0=y[:, i, :], scalar1=neg_mean[:, i : i + 1], scalar2=inv_std[:, i : i + 1],
+                    out=y[:, i, cols], in0=y[:, i, cols], scalar1=neg_mean[:, i : i + 1], scalar2=inv_std[:, i : i + 1],
                     op0=ALU.add, op1=ALU.mult,
                 )
-            pieces = [(i, slice(first, first + LN_PIECE)) for i in range(PAIR) for first in range(0, D, LN_PIECE)]
             for i, cols in pieces:
                 nc.gpsimd.tensor_tensor(out=y[:, i, cols], in0=y[:, i, cols], in1=gamma_bc[:, cols], op=ALU.mult)
             for i, cols in pieces:
@@ -300,22 +334,48 @@ def tile_multiheadattentionlayer_pa_t_kernel(
             rows = slice(a * PAIR * P, (a + 1) * PAIR * P)
             nc.sync.dma_start(out=out[b, rows, :].rearrange("(t p) d -> p t d", p=P), in_=y[:])
 
-        for j in range(len(steps) + 2):
-            if j < len(steps):
-                b, a, h = steps[j]
-                slot = H * a + h
-                if slot == 0:
-                    quantise_values(b)
-                    if b + 2 < B:
+        n_steps = len(steps)
+        for i in range(PAIR):
+            scores(0, i)
+        with tc.manual_schedule():
+            for j in range(n_steps + STATS_LAG + PAIR):
+                maxing = j < n_steps
+                exping = 0 <= j - EXP_LAG < n_steps
+                attending = 0 <= j - ATTEND_LAG < n_steps
+                preparing = maxing and steps[j][0] + 1 < B
+                if maxing:
+                    b, a, h = steps[j]
+                    slot = H * a + h
+                    if slot == 0 and b + 2 < B:
                         load_batch(b + 2)
-                scores_and_row_max(j)
-            if 1 <= j <= len(steps):
-                exponentials(j - 1)
-            if j < B:
-                row_mask(j)
-            if j < len(steps) and b + 1 < B:
-                prepare_slot(b + 1, slot)
-            if 1 <= j <= len(steps):
-                keys_of_e_onto_partitions(j - 1)
-            if j >= 2:
-                attend(j - 2)
+                if exping:
+                    exponentials(j - EXP_LAG)
+                if preparing:
+                    prepare_on_tensor(b + 1, slot)
+                for i in range(PAIR):
+                    if maxing:
+                        row_max(j, i)
+                    if j + 1 < n_steps:
+                        scores(j + 1, i)
+                    if attending and i == 0:
+                        invert_row_sums(j - ATTEND_LAG)
+                    if attending and i == 1:
+                        apply_mask(j - ATTEND_LAG)
+                if exping:
+                    keys_of_e_onto_partitions(j - EXP_LAG)
+                if attending:
+                    e_times_v(j - ATTEND_LAG)
+                if maxing and slot == 0:
+                    quantise_values(b)
+                if preparing:
+                    prepare_on_vector(b + 1, slot)
+                for i in range(PAIR):
+                    last = j - STATS_LAG - i
+                    if 0 <= last < n_steps and steps[last][2] == H - 1:
+                        done = y_of[steps[last][0], steps[last][1]]
+                        nc.vector.bn_stats(out=done["stats"][:, i, :], in_=done["y"][:, i, :])
+                if attending:
+                    add_residual(j - ATTEND_LAG)
+                last = j - STATS_LAG - (PAIR - 1)
+                if 0 <= last < n_steps and steps[last][2] == H - 1:
+                    layer_norm_and_store(steps[last][0], steps[last][1])

@@ -25,8 +25,9 @@ SCALE = 1.0 / DH ** 0.5
 LN_EPS = 1e-8
 LN_PIECE = 256
 EXP_LAG = 1
-ATTEND_LAG = 2
-STATS_LAG = 3
+COPY_LAG = 2
+ATTEND_LAG = 3
+STATS_LAG = 4
 
 FLOPS = 2 * B * S * DK * D + 2 * 2 * B * H * S * S * DH
 
@@ -39,41 +40,55 @@ def tile_multiheadattentionlayer_pa_t_kernel(
         const = ctx.enter_context(tc.tile_pool(name="const", bufs=1))
         loads = ctx.enter_context(tc.tile_pool(name="loads", bufs=2))
         ready = ctx.enter_context(tc.tile_pool(name="ready", bufs=2))
-        flow = ctx.enter_context(tc.tile_pool(name="flow", bufs=3))
+        flow = ctx.enter_context(tc.tile_pool(name="flow", bufs=4))
         score_ps = ctx.enter_context(tc.psum_pool(name="score_ps", bufs=2))
         et_ps = ctx.enter_context(tc.psum_pool(name="et_ps", bufs=2))
-        o_ps = ctx.enter_context(tc.psum_pool(name="o_ps", bufs=2))
-        prep_ps = ctx.enter_context(tc.psum_pool(name="prep_ps", bufs=2))
+        o_ps = ctx.enter_context(tc.psum_pool(name="o_ps", bufs=1))
+        v_ps = ctx.enter_context(tc.psum_pool(name="v_ps", bufs=1))
+        turn_ps = ctx.enter_context(tc.psum_pool(name="turn_ps", bufs=2))
 
-        batch = {}
+        batch = {b: {} for b in range(B)}
 
-        def load_batch(b):
-            keys_sb = loads.tile([P, TILES * DK], BF16, name="keys_sb")
+        def load_keys(b):
+            keys_sb = loads.tile([P, TILES * DK], BF16, name="keys_sb", bufs=3)
             nc.sync.dma_start(
                 out=keys_sb[:].rearrange("q (u x) -> q u x", u=2),
                 in_=keys[b].rearrange("(u q e) k -> q u (e k)", u=2, e=2),
             )
+            batch[b]["keys_sb"] = keys_sb
+
+        def load_heads(b):
             q_sb = loads.tile([P, TILES, D], BF16, name="q_sb")
             nc.sync.dma_start(out=q_sb[:], in_=q_relu[b].rearrange("(t p) d -> p t d", p=P))
             k_sb = loads.tile([P, TILES, D], BF16, name="k_sb")
             nc.sync.dma_start(out=k_sb[:], in_=k_relu[b].rearrange("(t p) d -> p t d", p=P))
-            batch[b] = {"keys_sb": keys_sb, "q_sb": q_sb, "k_sb": k_sb}
+            batch[b]["q_sb"] = q_sb
+            batch[b]["k_sb"] = k_sb
+
+        x_sb = const.tile([P, B, TILES, D], BF16, name="x_sb")
+
+        def load_queries(b):
+            nc.sync.dma_start(out=x_sb[:, b], in_=queries[b].rearrange("(t p) d -> p t d", p=P))
 
         wv_sb = const.tile([P, TILES * DK], BF16, name="wv_sb")
         nc.sync.dma_start(
             out=wv_sb[:].rearrange("p (t k) -> p t k", t=TILES), in_=Wv.rearrange("(t p) k -> p t k", p=P)
         )
-        load_batch(0)
+        load_keys(0)
+        load_heads(0)
+        load_keys(1)
         bias_bc = const.tile([P, D], BF16, name="bias_bc")
         nc.sync.dma_start(out=bias_bc[:], in_=bv.partition_broadcast(P))
-        x_sb = const.tile([P, B, TILES, D], BF16, name="x_sb")
-        for b in range(B):
-            nc.sync.dma_start(out=x_sb[:, b], in_=queries[b].rearrange("(t p) d -> p t d", p=P))
+        load_keys(2)
+        for b in range(B // 2):
+            load_queries(b)
+        load_heads(1)
+        for b in range(B // 2, B):
+            load_queries(b)
         gamma_raw = const.tile([P, D], BF16, name="gamma_raw")
         nc.sync.dma_start(out=gamma_raw[:], in_=ln_gamma.partition_broadcast(P))
         beta_raw = const.tile([P, D], BF16, name="beta_raw")
         nc.sync.dma_start(out=beta_raw[:], in_=ln_beta.partition_broadcast(P))
-        load_batch(1)
 
         ident_bf = const.tile([P, P], BF16, name="ident_bf")
         make_identity(nc, ident_bf[:])
@@ -82,13 +97,14 @@ def tile_multiheadattentionlayer_pa_t_kernel(
         neg_half = const.tile([P, PAIR], F32, name="neg_half")
         nc.gpsimd.memset(neg_half[:], -0.5)
         gamma_bc = const.tile([P, D], F32, name="gamma_bc")
-        nc.vector.tensor_copy(out=gamma_bc[:], in_=gamma_raw[:])
+        nc.gpsimd.tensor_copy(out=gamma_bc[:], in_=gamma_raw[:])
         beta_bc = const.tile([P, D], F32, name="beta_bc")
-        nc.vector.tensor_copy(out=beta_bc[:], in_=beta_raw[:])
+        nc.gpsimd.tensor_copy(out=beta_bc[:], in_=beta_raw[:])
+        mask01 = const.tile([P, B * TILES], F32, name="mask01")
 
         def pairs_onto_partitions(rows_sb, grouped, g, pair):
             words = rows_sb[:].bitcast(F32)
-            bank = prep_ps.tile([P, 2, PAIR * P], F32, name="words_t", tag="prep")
+            bank = turn_ps.tile([P, 2, PAIR * P], F32, name="words_t", tag="turn")
             for u in range(2):
                 for r in range(PAIR):
                     first = (PAIR * pair + r) * (DK // 2) + g * (K_PASS // 2) + u * P
@@ -104,24 +120,47 @@ def tile_multiheadattentionlayer_pa_t_kernel(
                 in_=grouped[:].bitcast(BF16)[:, g * S * PACK : (g + 1) * S * PACK],
             )
 
-        def heads_onto_partitions(rows_sb, heads_t, head_pair):
-            bank = prep_ps.tile([P, PAIR, S], BF16, name="heads_bank", tag="prep")
+        def keys_bank(b, part):
+            tiles = batch[b]
+            if part == 0:
+                tiles["keys_grouped"] = ready.tile([P, PASSES * S * 2], F32, name="keys_grouped", align_bytes=64)
+            pairs_onto_partitions(tiles["keys_sb"], tiles["keys_grouped"], part // 2, part % 2)
+
+        def quantise_keys(b, g):
+            tiles = batch[b]
+            if g == 0:
+                tiles["keys_codes"] = ready.tile([P, PASSES * S], U32, name="keys_codes", align_bytes=64)
+                tiles["keys_scales"] = ready.tile([P, PASSES * S], U8, name="keys_scales", align_bytes=64)
+            quantise_pass(tiles["keys_grouped"], tiles["keys_codes"], tiles["keys_scales"], g)
+
+        def heads_bank(b, part):
+            tiles = batch[b]
+            if part == 0:
+                tiles["q_t"] = ready.tile([P, H, S], BF16, name="q_t")
+                tiles["k_t"] = ready.tile([P, H, S], BF16, name="k_t")
+            rows_sb = tiles["q_sb"] if part % 2 == 0 else tiles["k_sb"]
+            heads_t = tiles["q_t"] if part % 2 == 0 else tiles["k_t"]
+            first_head = PAIR * (part // 2)
+            bank = turn_ps.tile([P, PAIR, S], BF16, name="heads_bank", tag="turn")
             for hh in range(PAIR):
-                h = PAIR * head_pair + hh
+                h = first_head + hh
                 for t in range(TILES):
                     nc.tensor.transpose(
                         bank[:, hh, t * P : (t + 1) * P], rows_sb[:, t, h * DH : (h + 1) * DH], ident_bf[:]
                     )
-            nc.scalar.copy(out=heads_t[:, PAIR * head_pair : PAIR * (head_pair + 1), :], in_=bank[:])
+            nc.scalar.copy(out=heads_t[:, first_head : first_head + PAIR, :], in_=bank[:])
 
-        def project_values(tiles, h):
-            bank = prep_ps.tile([P, TILES, DH], F32, name="v_bank", tag="prep")
-            for t in range(TILES):
+        def project_values(b, part):
+            tiles = batch[b]
+            h = part // 2
+            if part % 2 == 0:
+                tiles["v_bank"] = v_ps.tile([P, TILES, DH], F32, name="v_bank")
+            for t in range(PAIR * (part % 2), PAIR * (part % 2) + PAIR):
                 for g in range(PASSES):
                     key_cols = slice(g * S + t * P, g * S + (t + 1) * P)
                     out_cols = slice(g * D + h * DH, g * D + (h + 1) * DH)
                     nc.tensor.matmul_mx(
-                        out=bank[:, t, :],
+                        out=tiles["v_bank"][:, t, :],
                         lhsT=tiles["keys_codes"][:, key_cols].bitcast(FP8X4),
                         lhsT_scale=tiles["keys_scales"][:, key_cols],
                         rhs=wv_codes[:, out_cols].bitcast(FP8X4),
@@ -129,9 +168,11 @@ def tile_multiheadattentionlayer_pa_t_kernel(
                         start=(g == 0),
                         stop=(g == PASSES - 1),
                     )
-            tiles["v_bank"] = bank
 
-        def add_bias(tiles, h):
+        def add_bias(b, h):
+            tiles = batch[b]
+            if h == 0:
+                tiles["v_grouped"] = ready.tile([P, H, DH, PACK], BF16, name="v_grouped", align_bytes=64)
             nc.vector.tensor_tensor(
                 out=tiles["v_grouped"][:, h, :, :],
                 in0=tiles["v_bank"][:].rearrange("q t c -> q c t"),
@@ -139,38 +180,9 @@ def tile_multiheadattentionlayer_pa_t_kernel(
                 op=ALU.add,
             )
 
-        def prepare_on_tensor(b, slot):
-            tiles = batch[b]
-            if 3 <= slot < 7:
-                project_values(tiles, slot - 3)
-            if slot == 0:
-                tiles["keys_grouped"] = ready.tile([P, PASSES * S * 2], F32, name="keys_grouped", align_bytes=64)
-            if slot < 2:
-                for pair in range(TILES // PAIR):
-                    pairs_onto_partitions(tiles["keys_sb"], tiles["keys_grouped"], slot, pair)
-            if slot == 2:
-                tiles["q_t"] = ready.tile([P, H, S], BF16, name="q_t")
-            if 2 <= slot < 4:
-                heads_onto_partitions(tiles["q_sb"], tiles["q_t"], slot - 2)
-            if slot == 4:
-                tiles["k_t"] = ready.tile([P, H, S], BF16, name="k_t")
-            if 4 <= slot < 6:
-                heads_onto_partitions(tiles["k_sb"], tiles["k_t"], slot - 4)
-
-        def prepare_on_vector(b, slot):
-            tiles = batch[b]
-            if slot == 1:
-                tiles["keys_codes"] = ready.tile([P, PASSES * S], U32, name="keys_codes", align_bytes=64)
-                tiles["keys_scales"] = ready.tile([P, PASSES * S], U8, name="keys_scales", align_bytes=64)
-            if 1 <= slot < 3:
-                quantise_pass(tiles["keys_grouped"], tiles["keys_codes"], tiles["keys_scales"], slot - 1)
-            if slot == 3:
-                tiles["v_grouped"] = ready.tile([P, H, DH, PACK], BF16, name="v_grouped", align_bytes=64)
-            if 3 <= slot < 7:
-                add_bias(tiles, slot - 3)
-            if slot == 7:
-                v_flat = tiles["v_grouped"][:].rearrange("q h c t -> q (h c t)")
-                nc.vector.tensor_scalar_max(out=v_flat, in0=v_flat, scalar1=0.0)
+        def relu_values(b):
+            v_flat = batch[b]["v_grouped"][:].rearrange("q h c t -> q (h c t)")
+            nc.vector.tensor_scalar_max(out=v_flat, in0=v_flat, scalar1=0.0)
 
         def quantise_values(b):
             tiles = batch[b]
@@ -182,6 +194,14 @@ def tile_multiheadattentionlayer_pa_t_kernel(
                 in_=tiles["v_grouped"][:].rearrange("q h c t -> q (h c t)"),
             )
 
+        def row_mask(b):
+            for t in range(TILES):
+                unread = flow.tile([P, D], BF16, name="unread")
+                nc.vector.tensor_scalar(
+                    out=unread[:], in0=x_sb[:, b, t, :], scalar1=0.0, scalar2=None, op0=ALU.not_equal, op1=ALU.max,
+                    accum_out=mask01[:, b * TILES + t : b * TILES + t + 1],
+                )
+
         wv_grouped = const.tile([P, PASSES * D * 2], F32, name="wv_grouped", align_bytes=64)
         wv_codes = const.tile([P, PASSES * D], U32, name="wv_codes", align_bytes=64)
         wv_scales = const.tile([P, PASSES * D], U8, name="wv_scales", align_bytes=64)
@@ -190,31 +210,23 @@ def tile_multiheadattentionlayer_pa_t_kernel(
                 pairs_onto_partitions(wv_sb, wv_grouped, g, pair)
         for g in range(PASSES):
             quantise_pass(wv_grouped, wv_codes, wv_scales, g)
-        for slot in range(SLOTS):
-            prepare_on_tensor(0, slot)
-            prepare_on_vector(0, slot)
-
-        abs_sum = const.tile([P, B * TILES], F32, name="abs_sum")
-        mask01 = const.tile([P, B * TILES], F32, name="mask01")
-        for b in range(B):
-            cols = slice(b * TILES, (b + 1) * TILES)
-            if b % 2 == 0:
-                for t in range(TILES):
-                    unread = flow.tile([P, D], BF16, name="unread")
-                    nc.scalar.activation(
-                        out=unread[:], in_=x_sb[:, b, t, :], func=ACT.Abs,
-                        accum_out=abs_sum[:, b * TILES + t : b * TILES + t + 1],
-                    )
-                nc.vector.tensor_single_scalar(out=mask01[:, cols], in_=abs_sum[:, cols], scalar=0.0, op=ALU.is_gt)
-            else:
-                for t in range(TILES):
-                    unread = flow.tile([P, D], BF16, name="unread_v")
-                    nc.vector.tensor_scalar(
-                        out=unread[:], in0=x_sb[:, b, t, :], scalar1=0.0, scalar2=None, op0=ALU.not_equal, op1=ALU.max,
-                        accum_out=mask01[:, b * TILES + t : b * TILES + t + 1],
-                    )
+        for part in range(4):
+            keys_bank(0, part)
+        for g in range(PASSES):
+            quantise_keys(0, g)
+        for part in range(4):
+            heads_bank(0, part)
+        for part in range(SLOTS):
+            project_values(0, part)
+            if part % 2 == 1:
+                add_bias(0, part // 2)
+        for part in range(4):
+            keys_bank(1, part)
+        for g in range(PASSES):
+            quantise_keys(1, g)
 
         steps = [(b, a, h) for b in range(B) for a in range(HALVES) for h in range(H)]
+        n_steps = len(steps)
         live = {}
         y_of = {}
 
@@ -248,7 +260,7 @@ def tile_multiheadattentionlayer_pa_t_kernel(
                     scale=-1.0, bias=tiles["neg_max"][:, i : i + 1], accum_out=tiles["row_sum"][:, i : i + 1],
                 )
 
-        def keys_of_e_onto_partitions(j):
+        def transpose_e(j):
             tiles = live[j]
             words = tiles["e_sb"][:].bitcast(F32)
             bank = et_ps.tile([P, PAIR, 2, P], F32, name="et_bank")
@@ -256,24 +268,14 @@ def tile_multiheadattentionlayer_pa_t_kernel(
                 for u in range(2):
                     first = i * (S // 2) + u * P
                     nc.tensor.transpose(bank[:, i, u, :], words[:, first : first + P], ident_f32[:])
+            tiles["et_bank"] = bank
+
+        def copy_e(j):
+            tiles = live[j]
             tiles["e_grouped"] = flow.tile([P, PAIR * P * 2], F32, name="e_grouped", align_bytes=64)
             nc.scalar.copy(
                 out=tiles["e_grouped"][:].rearrange("q (i r u) -> q i r u", i=PAIR, u=2),
-                in_=bank[:].rearrange("q i u r -> q i r u"),
-            )
-
-        def invert_row_sums(j):
-            tiles = live[j]
-            tiles["inv_sum"] = flow.tile([P, PAIR], F32, name="inv_sum")
-            nc.vector.reciprocal(out=tiles["inv_sum"][:], in_=tiles["row_sum"][:])
-
-        def apply_mask(j):
-            b, a, h = steps[j]
-            tiles = live[j]
-            first = ((H * b + h) % B) * TILES + PAIR * a
-            tiles["row_scale"] = flow.tile([P, PAIR], F32, name="row_scale")
-            nc.vector.tensor_tensor(
-                out=tiles["row_scale"][:], in0=tiles["inv_sum"][:], in1=mask01[:, first : first + PAIR], op=ALU.mult
+                in_=tiles["et_bank"][:].rearrange("q i u r -> q i r u"),
             )
 
         def e_times_v(j):
@@ -294,6 +296,20 @@ def tile_multiheadattentionlayer_pa_t_kernel(
                     stop=True,
                 )
             tiles["o_bank"] = bank
+
+        def invert_row_sums(j):
+            tiles = live[j]
+            tiles["inv_sum"] = flow.tile([P, PAIR], F32, name="inv_sum")
+            nc.vector.reciprocal(out=tiles["inv_sum"][:], in_=tiles["row_sum"][:])
+
+        def apply_mask(j):
+            b, a, h = steps[j]
+            tiles = live[j]
+            first = ((H * b + h) % B) * TILES + PAIR * a
+            tiles["row_scale"] = flow.tile([P, PAIR], F32, name="row_scale")
+            nc.vector.tensor_tensor(
+                out=tiles["row_scale"][:], in0=tiles["inv_sum"][:], in1=mask01[:, first : first + PAIR], op=ALU.mult
+            )
 
         def add_residual(j):
             b, a, h = steps[j]
@@ -334,48 +350,65 @@ def tile_multiheadattentionlayer_pa_t_kernel(
             rows = slice(a * PAIR * P, (a + 1) * PAIR * P)
             nc.sync.dma_start(out=out[b, rows, :].rearrange("(t p) d -> p t d", p=P), in_=y[:])
 
-        n_steps = len(steps)
+        def is_step(j):
+            return 0 <= j < n_steps
+
+        def completes_rows(j):
+            return is_step(j) and steps[j][2] == H - 1
+
         for i in range(PAIR):
             scores(0, i)
         with tc.manual_schedule():
             for j in range(n_steps + STATS_LAG + PAIR):
-                maxing = j < n_steps
-                exping = 0 <= j - EXP_LAG < n_steps
-                attending = 0 <= j - ATTEND_LAG < n_steps
-                preparing = maxing and steps[j][0] + 1 < B
-                if maxing:
-                    b, a, h = steps[j]
-                    slot = H * a + h
-                    if slot == 0 and b + 2 < B:
-                        load_batch(b + 2)
-                if exping:
+                b = j // SLOTS
+                slot = j % SLOTS
+                if slot == 0 and b + 3 < B:
+                    load_keys(b + 3)
+                if slot == 0 and b + 2 < B:
+                    load_heads(b + 2)
+
+                if is_step(j - EXP_LAG):
                     exponentials(j - EXP_LAG)
-                if preparing:
-                    prepare_on_tensor(b + 1, slot)
-                for i in range(PAIR):
-                    if maxing:
-                        row_max(j, i)
-                    if j + 1 < n_steps:
-                        scores(j + 1, i)
-                    if attending and i == 0:
-                        invert_row_sums(j - ATTEND_LAG)
-                    if attending and i == 1:
-                        apply_mask(j - ATTEND_LAG)
-                if exping:
-                    keys_of_e_onto_partitions(j - EXP_LAG)
-                if attending:
+                if is_step(j - COPY_LAG):
+                    copy_e(j - COPY_LAG)
+                if slot < 4 and b + 2 < B:
+                    keys_bank(b + 2, slot)
+                if slot >= 4 and b + 1 < B:
+                    heads_bank(b + 1, slot - 4)
+
+                if is_step(j - ATTEND_LAG):
                     e_times_v(j - ATTEND_LAG)
-                if maxing and slot == 0:
-                    quantise_values(b)
-                if preparing:
-                    prepare_on_vector(b + 1, slot)
+                if b + 1 < B:
+                    project_values(b + 1, slot)
+
                 for i in range(PAIR):
-                    last = j - STATS_LAG - i
-                    if 0 <= last < n_steps and steps[last][2] == H - 1:
-                        done = y_of[steps[last][0], steps[last][1]]
+                    if is_step(j):
+                        row_max(j, i)
+                    if is_step(j + 1):
+                        scores(j + 1, i)
+                    if is_step(j - ATTEND_LAG) and i == 0:
+                        invert_row_sums(j - ATTEND_LAG)
+                    if is_step(j - ATTEND_LAG) and i == 1:
+                        apply_mask(j - ATTEND_LAG)
+                if is_step(j - EXP_LAG):
+                    transpose_e(j - EXP_LAG)
+
+                if slot % 2 == 1 and b + 1 < B:
+                    add_bias(b + 1, slot // 2)
+                if slot == 0 and b < B:
+                    relu_values(b)
+                if slot == 2 and b < B:
+                    quantise_values(b)
+                if slot >= 4 and slot % 2 == 0 and b + 2 < B:
+                    quantise_keys(b + 2, (slot - 4) // 2)
+                if j < B:
+                    row_mask(j)
+
+                for i in range(PAIR):
+                    if completes_rows(j - STATS_LAG - i):
+                        done = y_of[steps[j - STATS_LAG - i][0], steps[j - STATS_LAG - i][1]]
                         nc.vector.bn_stats(out=done["stats"][:, i, :], in_=done["y"][:, i, :])
-                if attending:
+                if is_step(j - ATTEND_LAG):
                     add_residual(j - ATTEND_LAG)
-                last = j - STATS_LAG - (PAIR - 1)
-                if 0 <= last < n_steps and steps[last][2] == H - 1:
-                    layer_norm_and_store(steps[last][0], steps[last][1])
+                if completes_rows(j - STATS_LAG - (PAIR - 1)):
+                    layer_norm_and_store(steps[j - STATS_LAG - (PAIR - 1)][0], steps[j - STATS_LAG - (PAIR - 1)][1])

@@ -52,8 +52,7 @@ def tile_multiheadattentionlayer_pa_t_kernel(
         def load_keys(b):
             keys_sb = loads.tile([P, TILES * DK], BF16, name="keys_sb", bufs=3)
             nc.sync.dma_start(
-                out=keys_sb[:].rearrange("q (u x) -> q u x", u=2),
-                in_=keys[b].rearrange("(u q e) k -> q u (e k)", u=2, e=2),
+                out=keys_sb[:].rearrange("p (t k) -> p t k", t=TILES), in_=keys[b].rearrange("(t p) k -> p t k", p=P)
             )
             batch[b]["keys_sb"] = keys_sb
 
@@ -70,6 +69,9 @@ def tile_multiheadattentionlayer_pa_t_kernel(
         def load_queries(b):
             nc.sync.dma_start(out=x_sb[:, b], in_=queries[b].rearrange("(t p) d -> p t d", p=P))
 
+        bias_rows = const.tile([P, P], BF16, name="bias_rows")
+        nc.vector.memset(bias_rows[:], 0.0)
+        nc.sync.dma_start(out=bias_rows[0:H, :], in_=bv.rearrange("(h c) -> h c", h=H))
         wv_sb = const.tile([P, TILES * DK], BF16, name="wv_sb")
         nc.sync.dma_start(
             out=wv_sb[:].rearrange("p (t k) -> p t k", t=TILES), in_=Wv.rearrange("(t p) k -> p t k", p=P)
@@ -77,8 +79,6 @@ def tile_multiheadattentionlayer_pa_t_kernel(
         load_keys(0)
         load_heads(0)
         load_keys(1)
-        bias_bc = const.tile([P, D], BF16, name="bias_bc")
-        nc.sync.dma_start(out=bias_bc[:], in_=bv.partition_broadcast(P))
         load_keys(2)
         for b in range(B // 2):
             load_queries(b)
@@ -102,16 +102,17 @@ def tile_multiheadattentionlayer_pa_t_kernel(
         nc.gpsimd.tensor_copy(out=beta_bc[:], in_=beta_raw[:])
         mask01 = const.tile([P, B * TILES], F32, name="mask01")
 
-        def pairs_onto_partitions(rows_sb, grouped, g, pair):
+        def transpose_pairs(rows_sb, row_words, first, pair, pool):
             words = rows_sb[:].bitcast(F32)
-            bank = turn_ps.tile([P, 2, PAIR * P], F32, name="words_t", tag="turn")
+            bank = pool.tile([P, 2, PAIR * P], F32, name="pairs_bank", tag="turn")
             for u in range(2):
                 for r in range(PAIR):
-                    first = (PAIR * pair + r) * (DK // 2) + g * (K_PASS // 2) + u * P
-                    nc.tensor.transpose(bank[:, u, r * P : (r + 1) * P], words[:, first : first + P], ident_f32[:])
-            dst = grouped[:].rearrange("q (g s u) -> q g s u", g=PASSES, u=2)
-            rows = slice(pair * PAIR * P, (pair + 1) * PAIR * P)
-            nc.scalar.copy(out=dst[:, g, rows, :], in_=bank[:].rearrange("q u s -> q s u"))
+                    col = (PAIR * pair + r) * row_words + first + u * P
+                    nc.tensor.transpose(bank[:, u, r * P : (r + 1) * P], words[:, col : col + P], ident_f32[:])
+            return bank
+
+        def copy_pairs(bank, grouped_rows):
+            nc.scalar.copy(out=grouped_rows, in_=bank[:].rearrange("q u s -> q s u"))
 
         def quantise_pass(grouped, codes, scales, g):
             nc.vector.quantize_mx(
@@ -120,11 +121,17 @@ def tile_multiheadattentionlayer_pa_t_kernel(
                 in_=grouped[:].bitcast(BF16)[:, g * S * PACK : (g + 1) * S * PACK],
             )
 
+        def rows_of(grouped, g, pair):
+            first = (g * TILES + pair * PAIR) * P * 2
+            return grouped[:, first : first + PAIR * P * 2].rearrange("q (s u) -> q s u", u=2)
+
         def keys_bank(b, part):
             tiles = batch[b]
             if part == 0:
                 tiles["keys_grouped"] = ready.tile([P, PASSES * S * 2], F32, name="keys_grouped", align_bytes=64)
-            pairs_onto_partitions(tiles["keys_sb"], tiles["keys_grouped"], part // 2, part % 2)
+            g, pair = part // 2, part % 2
+            bank = transpose_pairs(tiles["keys_sb"], DK // 2, g * (K_PASS // 2), pair, turn_ps)
+            copy_pairs(bank, rows_of(tiles["keys_grouped"], g, pair))
 
         def quantise_keys(b, g):
             tiles = batch[b]
@@ -150,49 +157,37 @@ def tile_multiheadattentionlayer_pa_t_kernel(
                     )
             nc.scalar.copy(out=heads_t[:, first_head : first_head + PAIR, :], in_=bank[:])
 
-        def project_values(b, part):
-            tiles = batch[b]
-            h = part // 2
-            if part % 2 == 0:
-                tiles["v_bank"] = v_ps.tile([P, TILES, DH], F32, name="v_bank")
-            for t in range(PAIR * (part % 2), PAIR * (part % 2) + PAIR):
-                for g in range(PASSES):
-                    key_cols = slice(g * S + t * P, g * S + (t + 1) * P)
-                    out_cols = slice(g * D + h * DH, g * D + (h + 1) * DH)
-                    nc.tensor.matmul_mx(
-                        out=tiles["v_bank"][:, t, :],
-                        lhsT=tiles["keys_codes"][:, key_cols].bitcast(FP8X4),
-                        lhsT_scale=tiles["keys_scales"][:, key_cols],
-                        rhs=wv_codes[:, out_cols].bitcast(FP8X4),
-                        rhs_scale=wv_scales[:, out_cols],
-                        start=(g == 0),
-                        stop=(g == PASSES - 1),
-                    )
-
-        def add_bias(b, h):
+        def project_values(b, h):
             tiles = batch[b]
             if h == 0:
-                tiles["v_grouped"] = ready.tile([P, H, DH, PACK], BF16, name="v_grouped", align_bytes=64)
-            nc.vector.tensor_tensor(
-                out=tiles["v_grouped"][:, h, :, :],
-                in0=tiles["v_bank"][:].rearrange("q t c -> q c t"),
-                in1=bias_bc[:, h * DH : (h + 1) * DH].unsqueeze(2).to_broadcast([P, DH, TILES]),
-                op=ALU.add,
-            )
+                tiles["v_t"] = ready.tile([P, H * S], BF16, name="v_t")
+            bank = v_ps.tile([P, S], F32, name="v_bank")
+            for g in range(PASSES):
+                out_cols = slice(g * D + h * DH, g * D + (h + 1) * DH)
+                key_cols = slice(g * S, (g + 1) * S)
+                nc.tensor.matmul_mx(
+                    out=bank[:],
+                    lhsT=wv_codes[:, out_cols].bitcast(FP8X4),
+                    lhsT_scale=wv_scales[:, out_cols],
+                    rhs=tiles["keys_codes"][:, key_cols].bitcast(FP8X4),
+                    rhs_scale=tiles["keys_scales"][:, key_cols],
+                    start=(g == 0),
+                    stop=(g == PASSES - 1),
+                )
+            nc.scalar.activation(out=tiles["v_t"][:, h * S : (h + 1) * S], in_=bank[:], func=ACT.Relu, bias=bias_col[:, h : h + 1])
 
-        def relu_values(b):
-            v_flat = batch[b]["v_grouped"][:].rearrange("q h c t -> q (h c t)")
-            nc.vector.tensor_scalar_max(out=v_flat, in0=v_flat, scalar1=0.0)
+        def values_bank(b, pair):
+            tiles = batch[b]
+            if pair == 0:
+                tiles["v_grouped"] = ready.tile([P, D * 2], F32, name="v_grouped", align_bytes=64)
+            bank = transpose_pairs(tiles["v_t"], S // 2, 0, pair, turn_ps)
+            copy_pairs(bank, rows_of(tiles["v_grouped"], 0, pair))
 
         def quantise_values(b):
             tiles = batch[b]
             tiles["v_codes"] = ready.tile([P, D], U32, name="v_codes", align_bytes=64)
             tiles["v_scales"] = ready.tile([P, D], U8, name="v_scales", align_bytes=64)
-            nc.vector.quantize_mx(
-                out=tiles["v_codes"][:].bitcast(FP8X4),
-                scales=tiles["v_scales"][:],
-                in_=tiles["v_grouped"][:].rearrange("q h c t -> q (h c t)"),
-            )
+            quantise_pass(tiles["v_grouped"], tiles["v_codes"], tiles["v_scales"], 0)
 
         def row_mask(b):
             for t in range(TILES):
@@ -207,7 +202,7 @@ def tile_multiheadattentionlayer_pa_t_kernel(
         wv_scales = const.tile([P, PASSES * D], U8, name="wv_scales", align_bytes=64)
         for g in range(PASSES):
             for pair in range(TILES // PAIR):
-                pairs_onto_partitions(wv_sb, wv_grouped, g, pair)
+                copy_pairs(transpose_pairs(wv_sb, DK // 2, g * (K_PASS // 2), pair, turn_ps), rows_of(wv_grouped, g, pair))
         for g in range(PASSES):
             quantise_pass(wv_grouped, wv_codes, wv_scales, g)
         for part in range(4):
@@ -216,10 +211,14 @@ def tile_multiheadattentionlayer_pa_t_kernel(
             quantise_keys(0, g)
         for part in range(4):
             heads_bank(0, part)
-        for part in range(SLOTS):
-            project_values(0, part)
-            if part % 2 == 1:
-                add_bias(0, part // 2)
+        bias_bank = turn_ps.tile([P, P], BF16, name="bias_bank", tag="turn")
+        nc.tensor.transpose(bias_bank[:], bias_rows[:], ident_bf[:])
+        bias_col = const.tile([P, H], F32, name="bias_col")
+        nc.vector.tensor_copy(out=bias_col[:], in_=bias_bank[:, 0:H])
+        for h in range(H):
+            project_values(0, h)
+        for pair in range(H // PAIR):
+            values_bank(0, pair)
         for part in range(4):
             keys_bank(1, part)
         for g in range(PASSES):
@@ -261,22 +260,12 @@ def tile_multiheadattentionlayer_pa_t_kernel(
                 )
 
         def transpose_e(j):
-            tiles = live[j]
-            words = tiles["e_sb"][:].bitcast(F32)
-            bank = et_ps.tile([P, PAIR, 2, P], F32, name="et_bank")
-            for i in range(PAIR):
-                for u in range(2):
-                    first = i * (S // 2) + u * P
-                    nc.tensor.transpose(bank[:, i, u, :], words[:, first : first + P], ident_f32[:])
-            tiles["et_bank"] = bank
+            live[j]["et_bank"] = transpose_pairs(live[j]["e_sb"], S // 2, 0, 0, et_ps)
 
         def copy_e(j):
             tiles = live[j]
             tiles["e_grouped"] = flow.tile([P, PAIR * P * 2], F32, name="e_grouped", align_bytes=64)
-            nc.scalar.copy(
-                out=tiles["e_grouped"][:].rearrange("q (i r u) -> q i r u", i=PAIR, u=2),
-                in_=tiles["et_bank"][:].rearrange("q i u r -> q i r u"),
-            )
+            copy_pairs(tiles["et_bank"], rows_of(tiles["e_grouped"], 0, 0))
 
         def e_times_v(j):
             b, a, h = steps[j]
@@ -337,16 +326,28 @@ def tile_multiheadattentionlayer_pa_t_kernel(
             nc.gpsimd.tensor_scalar(out=neg_mean[:], in0=mean_var[:, :, 0], scalar1=-1.0, scalar2=0.0, op0=ALU.mult, op1=ALU.add)
             inv_std = flow.tile([P, PAIR], F32, name="inv_std")
             nc.gpsimd.tensor_tensor(out=inv_std[:], in0=var_eps[:], in1=neg_half[:], op=ALU.pow)
-            pieces = [(i, slice(first, first + LN_PIECE)) for i in range(PAIR) for first in range(0, D, LN_PIECE)]
-            for i, cols in pieces:
-                nc.gpsimd.tensor_scalar(
-                    out=y[:, i, cols], in0=y[:, i, cols], scalar1=neg_mean[:, i : i + 1], scalar2=inv_std[:, i : i + 1],
-                    op0=ALU.add, op1=ALU.mult,
-                )
-            for i, cols in pieces:
-                nc.gpsimd.tensor_tensor(out=y[:, i, cols], in0=y[:, i, cols], in1=gamma_bc[:, cols], op=ALU.mult)
-            for i, cols in pieces:
-                nc.gpsimd.tensor_tensor(out=y[:, i, cols], in0=y[:, i, cols], in1=beta_bc[:, cols], op=ALU.add)
+            if (b, a) != steps[-1][0:2]:
+                pieces = [(i, slice(first, first + LN_PIECE)) for i in range(PAIR) for first in range(0, D, LN_PIECE)]
+                for i, cols in pieces:
+                    nc.gpsimd.tensor_scalar(
+                        out=y[:, i, cols], in0=y[:, i, cols], scalar1=neg_mean[:, i : i + 1],
+                        scalar2=inv_std[:, i : i + 1], op0=ALU.add, op1=ALU.mult,
+                    )
+                for i, cols in pieces:
+                    nc.gpsimd.tensor_tensor(out=y[:, i, cols], in0=y[:, i, cols], in1=gamma_bc[:, cols], op=ALU.mult)
+                for i, cols in pieces:
+                    nc.gpsimd.tensor_tensor(out=y[:, i, cols], in0=y[:, i, cols], in1=beta_bc[:, cols], op=ALU.add)
+            else:
+                for i in range(PAIR):
+                    nc.vector.scalar_tensor_tensor(
+                        out=y[:, i, :], in0=y[:, i, :], scalar=neg_mean[:, i : i + 1], in1=gamma_bc[:],
+                        op0=ALU.add, op1=ALU.mult,
+                    )
+                for i in range(PAIR):
+                    nc.vector.scalar_tensor_tensor(
+                        out=y[:, i, :], in0=y[:, i, :], scalar=inv_std[:, i : i + 1], in1=beta_bc[:],
+                        op0=ALU.mult, op1=ALU.add,
+                    )
             rows = slice(a * PAIR * P, (a + 1) * PAIR * P)
             nc.sync.dma_start(out=out[b, rows, :].rearrange("(t p) d -> p t d", p=P), in_=y[:])
 
@@ -375,11 +376,13 @@ def tile_multiheadattentionlayer_pa_t_kernel(
                     keys_bank(b + 2, slot)
                 if slot >= 4 and b + 1 < B:
                     heads_bank(b + 1, slot - 4)
+                if slot >= 5 and slot % 2 == 1 and b + 1 < B:
+                    values_bank(b + 1, (slot - 5) // 2)
 
                 if is_step(j - ATTEND_LAG):
                     e_times_v(j - ATTEND_LAG)
-                if b + 1 < B:
-                    project_values(b + 1, slot)
+                if slot % 2 == 0 and b + 1 < B:
+                    project_values(b + 1, slot // 2)
 
                 for i in range(PAIR):
                     if is_step(j):
@@ -393,14 +396,10 @@ def tile_multiheadattentionlayer_pa_t_kernel(
                 if is_step(j - EXP_LAG):
                     transpose_e(j - EXP_LAG)
 
-                if slot % 2 == 1 and b + 1 < B:
-                    add_bias(b + 1, slot // 2)
                 if slot == 0 and b < B:
-                    relu_values(b)
-                if slot == 2 and b < B:
                     quantise_values(b)
-                if slot >= 4 and slot % 2 == 0 and b + 2 < B:
-                    quantise_keys(b + 2, (slot - 4) // 2)
+                if slot in (2, 4) and b + 2 < B:
+                    quantise_keys(b + 2, (slot - 2) // 2)
                 if j < B:
                     row_mask(j)
 

@@ -155,7 +155,7 @@ def tile_multiheadattentionlayer_pa_t_kernel(
                     nc.tensor.transpose(
                         bank[:, hh, t * P : (t + 1) * P], rows_sb[:, t, h * DH : (h + 1) * DH], ident_bf[:]
                     )
-            nc.scalar.copy(out=heads_t[:, first_head : first_head + PAIR, :], in_=bank[:])
+            return bank, heads_t[:, first_head : first_head + PAIR, :]
 
         def project_values(b, h):
             tiles = batch[b]
@@ -210,7 +210,8 @@ def tile_multiheadattentionlayer_pa_t_kernel(
         for g in range(PASSES):
             quantise_keys(0, g)
         for part in range(4):
-            heads_bank(0, part)
+            bank, heads = heads_bank(0, part)
+            nc.scalar.copy(out=heads, in_=bank[:])
         bias_bank = turn_ps.tile([P, P], BF16, name="bias_bank", tag="turn")
         nc.tensor.transpose(bias_bank[:], bias_rows[:], ident_bf[:])
         bias_col = const.tile([P, H], F32, name="bias_col")
@@ -252,11 +253,14 @@ def tile_multiheadattentionlayer_pa_t_kernel(
         def exponentials(j):
             tiles = live[j]
             tiles["e_sb"] = flow.tile([P, PAIR * S], BF16, name="e_sb")
-            tiles["row_sum"] = flow.tile([P, PAIR], F32, name="row_sum")
+            if j % 2 == 0:
+                tiles["row_sum"] = flow.tile([P, 2, PAIR], F32, name="row_sum")
+            else:
+                tiles["row_sum"] = live[j - 1]["row_sum"]
             for i in range(PAIR):
                 nc.scalar.activation(
                     out=tiles["e_sb"][:, i * S : (i + 1) * S], in_=tiles["neg_s", i][:], func=ACT.Exp,
-                    scale=-1.0, bias=tiles["neg_max"][:, i : i + 1], accum_out=tiles["row_sum"][:, i : i + 1],
+                    scale=-1.0, bias=tiles["neg_max"][:, i : i + 1], accum_out=tiles["row_sum"][:, j % 2, i : i + 1],
                 )
 
         def transpose_e(j):
@@ -288,17 +292,19 @@ def tile_multiheadattentionlayer_pa_t_kernel(
 
         def invert_row_sums(j):
             tiles = live[j]
-            tiles["inv_sum"] = flow.tile([P, PAIR], F32, name="inv_sum")
+            tiles["inv_sum"] = flow.tile([P, 2, PAIR], F32, name="inv_sum")
             nc.vector.reciprocal(out=tiles["inv_sum"][:], in_=tiles["row_sum"][:])
 
         def apply_mask(j):
             b, a, h = steps[j]
-            tiles = live[j]
-            first = ((H * b + h) % B) * TILES + PAIR * a
-            tiles["row_scale"] = flow.tile([P, PAIR], F32, name="row_scale")
+            first = ((H * b + h) % B) * TILES
+            two_batches = mask01[:, first : first + 2 * TILES].rearrange("p (n t) -> p n t", n=2)
+            row_scale = flow.tile([P, 2, PAIR], F32, name="row_scale")
             nc.vector.tensor_tensor(
-                out=tiles["row_scale"][:], in0=tiles["inv_sum"][:], in1=mask01[:, first : first + PAIR], op=ALU.mult
+                out=row_scale[:], in0=live[j]["inv_sum"][:], in1=two_batches[:, :, PAIR * a : PAIR * (a + 1)], op=ALU.mult
             )
+            live[j]["row_scale"] = row_scale
+            live[j + 1]["row_scale"] = row_scale
 
         def add_residual(j):
             b, a, h = steps[j]
@@ -311,11 +317,11 @@ def tile_multiheadattentionlayer_pa_t_kernel(
             for i in range(PAIR):
                 nc.vector.scalar_tensor_tensor(
                     out=y_of[b, a]["y"][:, i, h * DH : (h + 1) * DH], in0=tiles["o_bank"][:, i, :],
-                    scalar=tiles["row_scale"][:, i : i + 1], in1=x_sb[:, b, PAIR * a + i, h * DH : (h + 1) * DH],
+                    scalar=tiles["row_scale"][:, j % 2, i : i + 1], in1=x_sb[:, b, PAIR * a + i, h * DH : (h + 1) * DH],
                     op0=ALU.mult, op1=ALU.add,
                 )
 
-        def layer_norm_and_store(b, a):
+        def layer_norm_and_store(b, a, on_vector):
             y = y_of[b, a]["y"]
             mean_var = flow.tile([P, PAIR, 2], F32, name="mean_var")
             for i in range(PAIR):
@@ -326,13 +332,13 @@ def tile_multiheadattentionlayer_pa_t_kernel(
             nc.gpsimd.tensor_scalar(out=neg_mean[:], in0=mean_var[:, :, 0], scalar1=-1.0, scalar2=0.0, op0=ALU.mult, op1=ALU.add)
             inv_std = flow.tile([P, PAIR], F32, name="inv_std")
             nc.gpsimd.tensor_tensor(out=inv_std[:], in0=var_eps[:], in1=neg_half[:], op=ALU.pow)
-            if (b, a) != steps[-1][0:2]:
-                pieces = [(i, slice(first, first + LN_PIECE)) for i in range(PAIR) for first in range(0, D, LN_PIECE)]
-                for i, cols in pieces:
+            if not on_vector:
+                for i in range(PAIR):
                     nc.gpsimd.tensor_scalar(
-                        out=y[:, i, cols], in0=y[:, i, cols], scalar1=neg_mean[:, i : i + 1],
+                        out=y[:, i, :], in0=y[:, i, :], scalar1=neg_mean[:, i : i + 1],
                         scalar2=inv_std[:, i : i + 1], op0=ALU.add, op1=ALU.mult,
                     )
+                pieces = [(i, slice(first, first + LN_PIECE)) for i in range(PAIR) for first in range(0, D, LN_PIECE)]
                 for i, cols in pieces:
                     nc.gpsimd.tensor_tensor(out=y[:, i, cols], in0=y[:, i, cols], in1=gamma_bc[:, cols], op=ALU.mult)
                 for i, cols in pieces:
@@ -348,8 +354,9 @@ def tile_multiheadattentionlayer_pa_t_kernel(
                         out=y[:, i, :], in0=y[:, i, :], scalar=inv_std[:, i : i + 1], in1=beta_bc[:],
                         op0=ALU.mult, op1=ALU.add,
                     )
-            rows = slice(a * PAIR * P, (a + 1) * PAIR * P)
-            nc.sync.dma_start(out=out[b, rows, :].rearrange("(t p) d -> p t d", p=P), in_=y[:])
+            for i in range(PAIR):
+                first = (a * PAIR + i) * P
+                nc.sync.dma_start(out=out[b, first : first + P, :], in_=y[:, i, :])
 
         def is_step(j):
             return 0 <= j < n_steps
@@ -375,7 +382,9 @@ def tile_multiheadattentionlayer_pa_t_kernel(
                 if slot < 4 and b + 2 < B:
                     keys_bank(b + 2, slot)
                 if slot >= 4 and b + 1 < B:
-                    heads_bank(b + 1, slot - 4)
+                    heads_ps, heads = heads_bank(b + 1, slot - 4)
+                    if slot % 2 == 0:
+                        nc.scalar.copy(out=heads, in_=heads_ps[:])
                 if slot >= 5 and slot % 2 == 1 and b + 1 < B:
                     values_bank(b + 1, (slot - 5) // 2)
 
@@ -389,13 +398,16 @@ def tile_multiheadattentionlayer_pa_t_kernel(
                         row_max(j, i)
                     if is_step(j + 1):
                         scores(j + 1, i)
-                    if is_step(j - ATTEND_LAG) and i == 0:
-                        invert_row_sums(j - ATTEND_LAG)
-                    if is_step(j - ATTEND_LAG) and i == 1:
-                        apply_mask(j - ATTEND_LAG)
+                    if is_step(j - ATTEND_LAG) and (j - ATTEND_LAG) % 2 == 0:
+                        if i == 0:
+                            invert_row_sums(j - ATTEND_LAG)
+                        else:
+                            apply_mask(j - ATTEND_LAG)
                 if is_step(j - EXP_LAG):
                     transpose_e(j - EXP_LAG)
 
+                if slot >= 4 and slot % 2 == 1 and b + 1 < B:
+                    nc.vector.tensor_copy(out=heads, in_=heads_ps[:])
                 if slot == 0 and b < B:
                     quantise_values(b)
                 if slot in (2, 4) and b + 2 < B:
@@ -410,4 +422,6 @@ def tile_multiheadattentionlayer_pa_t_kernel(
                 if is_step(j - ATTEND_LAG):
                     add_residual(j - ATTEND_LAG)
                 if completes_rows(j - STATS_LAG - (PAIR - 1)):
-                    layer_norm_and_store(steps[j - STATS_LAG - (PAIR - 1)][0], steps[j - STATS_LAG - (PAIR - 1)][1])
+                    layer_norm_and_store(
+                        steps[j - STATS_LAG - (PAIR - 1)][0], steps[j - STATS_LAG - (PAIR - 1)][1], on_vector=j >= n_steps
+                    )

@@ -96,6 +96,8 @@ def tile_multiheadattentionlayer_pa_t_kernel(
         make_identity(nc, ident_f32[:])
         neg_half = const.tile([P, PAIR], F32, name="neg_half")
         nc.gpsimd.memset(neg_half[:], -0.5)
+        eps_col = const.tile([P, 1], F32, name="eps_col")
+        nc.gpsimd.memset(eps_col[:], LN_EPS)
         gamma_bc = const.tile([P, D], F32, name="gamma_bc")
         nc.gpsimd.tensor_copy(out=gamma_bc[:], in_=gamma_raw[:])
         beta_bc = const.tile([P, D], F32, name="beta_bc")
@@ -157,16 +159,18 @@ def tile_multiheadattentionlayer_pa_t_kernel(
                     )
             return bank, heads_t[:, first_head : first_head + PAIR, :]
 
-        def project_values(b, h):
+        def project_values(b, part):
             tiles = batch[b]
-            if h == 0:
+            h, half = part // 2, part % 2
+            if part == 0:
                 tiles["v_t"] = ready.tile([P, H * S], BF16, name="v_t")
-            bank = v_ps.tile([P, S], F32, name="v_bank")
+            if half == 0:
+                tiles["v_bank"] = v_ps.tile([P, S], F32, name="v_bank")
             for g in range(PASSES):
                 out_cols = slice(g * D + h * DH, g * D + (h + 1) * DH)
-                key_cols = slice(g * S, (g + 1) * S)
+                key_cols = slice(g * S + half * (S // 2), g * S + (half + 1) * (S // 2))
                 nc.tensor.matmul_mx(
-                    out=bank[:],
+                    out=tiles["v_bank"][:, half * (S // 2) : (half + 1) * (S // 2)],
                     lhsT=wv_codes[:, out_cols].bitcast(FP8X4),
                     lhsT_scale=wv_scales[:, out_cols],
                     rhs=tiles["keys_codes"][:, key_cols].bitcast(FP8X4),
@@ -174,7 +178,10 @@ def tile_multiheadattentionlayer_pa_t_kernel(
                     start=(g == 0),
                     stop=(g == PASSES - 1),
                 )
-            nc.scalar.activation(out=tiles["v_t"][:, h * S : (h + 1) * S], in_=bank[:], func=ACT.Relu, bias=bias_col[:, h : h + 1])
+            if half == 1:
+                nc.scalar.activation(
+                    out=tiles["v_t"][:, h * S : (h + 1) * S], in_=tiles["v_bank"][:], func=ACT.Relu, bias=bias_col[:, h : h + 1]
+                )
 
         def values_bank(b, pair):
             tiles = batch[b]
@@ -216,10 +223,9 @@ def tile_multiheadattentionlayer_pa_t_kernel(
         nc.tensor.transpose(bias_bank[:], bias_rows[:], ident_bf[:])
         bias_col = const.tile([P, H], F32, name="bias_col")
         nc.vector.tensor_copy(out=bias_col[:], in_=bias_bank[:, 0:H])
-        for h in range(H):
-            project_values(0, h)
-        for pair in range(H // PAIR):
-            values_bank(0, pair)
+        for part in range(SLOTS):
+            project_values(0, part)
+        values_bank(0, 0)
         for part in range(4):
             keys_bank(1, part)
         for g in range(PASSES):
@@ -326,13 +332,17 @@ def tile_multiheadattentionlayer_pa_t_kernel(
             mean_var = flow.tile([P, PAIR, 2], F32, name="mean_var")
             for i in range(PAIR):
                 nc.vector.bn_aggr(out=mean_var[:, i, :], in_=y_of[b, a]["stats"][:, i, :])
-            var_eps = flow.tile([P, PAIR], F32, name="var_eps")
-            nc.gpsimd.tensor_scalar(out=var_eps[:], in0=mean_var[:, :, 1], scalar1=LN_EPS, scalar2=1.0, op0=ALU.add, op1=ALU.mult)
-            neg_mean = flow.tile([P, PAIR], F32, name="neg_mean")
-            nc.gpsimd.tensor_scalar(out=neg_mean[:], in0=mean_var[:, :, 0], scalar1=-1.0, scalar2=0.0, op0=ALU.mult, op1=ALU.add)
             inv_std = flow.tile([P, PAIR], F32, name="inv_std")
-            nc.gpsimd.tensor_tensor(out=inv_std[:], in0=var_eps[:], in1=neg_half[:], op=ALU.pow)
             if not on_vector:
+                var_eps = flow.tile([P, PAIR], F32, name="var_eps")
+                nc.gpsimd.tensor_scalar(
+                    out=var_eps[:], in0=mean_var[:, :, 1], scalar1=LN_EPS, scalar2=1.0, op0=ALU.add, op1=ALU.mult
+                )
+                neg_mean = flow.tile([P, PAIR], F32, name="neg_mean")
+                nc.gpsimd.tensor_scalar(
+                    out=neg_mean[:], in0=mean_var[:, :, 0], scalar1=-1.0, scalar2=0.0, op0=ALU.mult, op1=ALU.add
+                )
+                nc.gpsimd.tensor_tensor(out=inv_std[:], in0=var_eps[:], in1=neg_half[:], op=ALU.pow)
                 for i in range(PAIR):
                     nc.gpsimd.tensor_scalar(
                         out=y[:, i, :], in0=y[:, i, :], scalar1=neg_mean[:, i : i + 1],
@@ -344,11 +354,14 @@ def tile_multiheadattentionlayer_pa_t_kernel(
                 for i, cols in pieces:
                     nc.gpsimd.tensor_tensor(out=y[:, i, cols], in0=y[:, i, cols], in1=beta_bc[:, cols], op=ALU.add)
             else:
+                std = flow.tile([P, PAIR], F32, name="std")
+                nc.scalar.activation(out=std[:], in_=mean_var[:, :, 1], func=ACT.Sqrt, bias=eps_col[:])
                 for i in range(PAIR):
                     nc.vector.scalar_tensor_tensor(
-                        out=y[:, i, :], in0=y[:, i, :], scalar=neg_mean[:, i : i + 1], in1=gamma_bc[:],
-                        op0=ALU.add, op1=ALU.mult,
+                        out=y[:, i, :], in0=y[:, i, :], scalar=mean_var[:, i, 0:1], in1=gamma_bc[:],
+                        op0=ALU.subtract, op1=ALU.mult,
                     )
+                nc.vector.reciprocal(out=inv_std[:], in_=std[:])
                 for i in range(PAIR):
                     nc.vector.scalar_tensor_tensor(
                         out=y[:, i, :], in0=y[:, i, :], scalar=inv_std[:, i : i + 1], in1=beta_bc[:],
@@ -385,13 +398,15 @@ def tile_multiheadattentionlayer_pa_t_kernel(
                     heads_ps, heads = heads_bank(b + 1, slot - 4)
                     if slot % 2 == 0:
                         nc.scalar.copy(out=heads, in_=heads_ps[:])
-                if slot >= 5 and slot % 2 == 1 and b + 1 < B:
-                    values_bank(b + 1, (slot - 5) // 2)
+                if slot == 5 and b + 1 < B:
+                    values_bank(b + 1, 0)
+                if slot == 0 and b < B:
+                    values_bank(b, 1)
 
                 if is_step(j - ATTEND_LAG):
                     e_times_v(j - ATTEND_LAG)
-                if slot % 2 == 0 and b + 1 < B:
-                    project_values(b + 1, slot // 2)
+                if b + 1 < B:
+                    project_values(b + 1, slot)
 
                 for i in range(PAIR):
                     if is_step(j):
@@ -408,7 +423,7 @@ def tile_multiheadattentionlayer_pa_t_kernel(
 
                 if slot >= 4 and slot % 2 == 1 and b + 1 < B:
                     nc.vector.tensor_copy(out=heads, in_=heads_ps[:])
-                if slot == 0 and b < B:
+                if slot == 1 and b < B:
                     quantise_values(b)
                 if slot in (2, 4) and b + 2 < B:
                     quantise_keys(b + 2, (slot - 2) // 2)

@@ -23,6 +23,8 @@ HALVES = TILES // PAIR
 SLOTS = HALVES * H
 SCALE = 1.0 / DH ** 0.5
 LN_EPS = 1e-8
+WARM_FIRST = 6
+WARM_EACH = 1
 LN_PIECE = 256
 EXP_LAG = 1
 COPY_LAG = 2
@@ -49,11 +51,17 @@ def tile_multiheadattentionlayer_pa_t_kernel(
 
         batch = {b: {} for b in range(B)}
 
+        def load_row_pairs(rows_sb, rows):
+            for pair in range(TILES // PAIR):
+                tiles = slice(PAIR * pair, PAIR * (pair + 1))
+                nc.sync.dma_start(
+                    out=rows_sb[:].rearrange("p (t k) -> p t k", t=TILES)[:, tiles, :],
+                    in_=rows.rearrange("(t p) k -> p t k", p=P)[:, tiles, :],
+                )
+
         def load_keys(b):
             keys_sb = loads.tile([P, TILES * DK], BF16, name="keys_sb", bufs=3)
-            nc.sync.dma_start(
-                out=keys_sb[:].rearrange("p (t k) -> p t k", t=TILES), in_=keys[b].rearrange("(t p) k -> p t k", p=P)
-            )
+            load_row_pairs(keys_sb, keys[b])
             batch[b]["keys_sb"] = keys_sb
 
         def load_heads(b):
@@ -69,26 +77,26 @@ def tile_multiheadattentionlayer_pa_t_kernel(
         def load_queries(b):
             nc.sync.dma_start(out=x_sb[:, b], in_=queries[b].rearrange("(t p) d -> p t d", p=P))
 
+        zeros = const.tile([P, S], BF16, name="zeros")
+        nc.vector.memset(zeros[:], 0.0)
         bias_rows = const.tile([P, P], BF16, name="bias_rows")
         nc.vector.memset(bias_rows[:], 0.0)
-        nc.sync.dma_start(out=bias_rows[0:H, :], in_=bv.rearrange("(h c) -> h c", h=H))
         wv_sb = const.tile([P, TILES * DK], BF16, name="wv_sb")
-        nc.sync.dma_start(
-            out=wv_sb[:].rearrange("p (t k) -> p t k", t=TILES), in_=Wv.rearrange("(t p) k -> p t k", p=P)
-        )
+        load_row_pairs(wv_sb, Wv)
         load_keys(0)
+        nc.sync.dma_start(out=bias_rows[0:H, :], in_=bv.rearrange("(h c) -> h c", h=H))
         load_heads(0)
         load_keys(1)
-        load_keys(2)
         for b in range(B // 2):
             load_queries(b)
+        load_keys(2)
         load_heads(1)
         for b in range(B // 2, B):
             load_queries(b)
-        gamma_raw = const.tile([P, D], BF16, name="gamma_raw")
-        nc.sync.dma_start(out=gamma_raw[:], in_=ln_gamma.partition_broadcast(P))
-        beta_raw = const.tile([P, D], BF16, name="beta_raw")
-        nc.sync.dma_start(out=beta_raw[:], in_=ln_beta.partition_broadcast(P))
+        gamma_bc = const.tile([P, D], BF16, name="gamma_bc")
+        nc.sync.dma_start(out=gamma_bc[:], in_=ln_gamma.partition_broadcast(P))
+        beta_bc = const.tile([P, D], BF16, name="beta_bc")
+        nc.sync.dma_start(out=beta_bc[:], in_=ln_beta.partition_broadcast(P))
 
         ident_bf = const.tile([P, P], BF16, name="ident_bf")
         make_identity(nc, ident_bf[:])
@@ -98,23 +106,25 @@ def tile_multiheadattentionlayer_pa_t_kernel(
         nc.gpsimd.memset(neg_half[:], -0.5)
         eps_col = const.tile([P, 1], F32, name="eps_col")
         nc.gpsimd.memset(eps_col[:], LN_EPS)
-        gamma_bc = const.tile([P, D], F32, name="gamma_bc")
-        nc.gpsimd.tensor_copy(out=gamma_bc[:], in_=gamma_raw[:])
-        beta_bc = const.tile([P, D], F32, name="beta_bc")
-        nc.gpsimd.tensor_copy(out=beta_bc[:], in_=beta_raw[:])
         mask01 = const.tile([P, B * TILES], F32, name="mask01")
 
-        def transpose_pairs(rows_sb, row_words, first, pair, pool):
+        def transpose_pairs(rows_sb, row_words, first, pair, pool, tag):
             words = rows_sb[:].bitcast(F32)
-            bank = pool.tile([P, 2, PAIR * P], F32, name="pairs_bank", tag="turn")
+            bank = pool.tile([P, 2, PAIR * P], F32, name="pairs_bank", tag=tag)
             for u in range(2):
                 for r in range(PAIR):
                     col = (PAIR * pair + r) * row_words + first + u * P
                     nc.tensor.transpose(bank[:, u, r * P : (r + 1) * P], words[:, col : col + P], ident_f32[:])
             return bank
 
-        def copy_pairs(bank, grouped_rows):
-            nc.scalar.copy(out=grouped_rows, in_=bank[:].rearrange("q u s -> q s u"))
+        def copy_out(out, in_, on_vector):
+            if on_vector:
+                nc.vector.tensor_copy(out=out, in_=in_)
+            else:
+                nc.scalar.copy(out=out, in_=in_)
+
+        def copy_pairs(bank, grouped_rows, on_vector=False):
+            copy_out(grouped_rows, bank[:].rearrange("q u s -> q s u"), on_vector)
 
         def quantise_pass(grouped, codes, scales, g):
             nc.vector.quantize_mx(
@@ -127,13 +137,12 @@ def tile_multiheadattentionlayer_pa_t_kernel(
             first = (g * TILES + pair * PAIR) * P * 2
             return grouped[:, first : first + PAIR * P * 2].rearrange("q (s u) -> q s u", u=2)
 
-        def keys_bank(b, part):
+        def keys_bank(b, g, pair, pool=turn_ps, tag="turn", on_vector=False):
             tiles = batch[b]
-            if part == 0:
+            if "keys_grouped" not in tiles:
                 tiles["keys_grouped"] = ready.tile([P, PASSES * S * 2], F32, name="keys_grouped", align_bytes=64)
-            g, pair = part // 2, part % 2
-            bank = transpose_pairs(tiles["keys_sb"], DK // 2, g * (K_PASS // 2), pair, turn_ps)
-            copy_pairs(bank, rows_of(tiles["keys_grouped"], g, pair))
+            bank = transpose_pairs(tiles["keys_sb"], DK // 2, g * (K_PASS // 2), pair, pool, tag)
+            copy_pairs(bank, rows_of(tiles["keys_grouped"], g, pair), on_vector)
 
         def quantise_keys(b, g):
             tiles = batch[b]
@@ -142,7 +151,7 @@ def tile_multiheadattentionlayer_pa_t_kernel(
                 tiles["keys_scales"] = ready.tile([P, PASSES * S], U8, name="keys_scales", align_bytes=64)
             quantise_pass(tiles["keys_grouped"], tiles["keys_codes"], tiles["keys_scales"], g)
 
-        def heads_bank(b, part):
+        def heads_bank(b, part, pool=turn_ps, tag="turn"):
             tiles = batch[b]
             if part == 0:
                 tiles["q_t"] = ready.tile([P, H, S], BF16, name="q_t")
@@ -150,7 +159,7 @@ def tile_multiheadattentionlayer_pa_t_kernel(
             rows_sb = tiles["q_sb"] if part % 2 == 0 else tiles["k_sb"]
             heads_t = tiles["q_t"] if part % 2 == 0 else tiles["k_t"]
             first_head = PAIR * (part // 2)
-            bank = turn_ps.tile([P, PAIR, S], BF16, name="heads_bank", tag="turn")
+            bank = pool.tile([P, PAIR, S], BF16, name="heads_bank", tag=tag)
             for hh in range(PAIR):
                 h = first_head + hh
                 for t in range(TILES):
@@ -159,13 +168,13 @@ def tile_multiheadattentionlayer_pa_t_kernel(
                     )
             return bank, heads_t[:, first_head : first_head + PAIR, :]
 
-        def project_values(b, part):
+        def project_values(b, part, pool=v_ps, tag="v_bank", on_vector=False):
             tiles = batch[b]
             h, half = part // 2, part % 2
             if part == 0:
                 tiles["v_t"] = ready.tile([P, H * S], BF16, name="v_t")
             if half == 0:
-                tiles["v_bank"] = v_ps.tile([P, S], F32, name="v_bank")
+                tiles["v_bank"] = pool.tile([P, S], F32, name="v_bank", tag=tag)
             for g in range(PASSES):
                 out_cols = slice(g * D + h * DH, g * D + (h + 1) * DH)
                 key_cols = slice(g * S + half * (S // 2), g * S + (half + 1) * (S // 2))
@@ -179,15 +188,19 @@ def tile_multiheadattentionlayer_pa_t_kernel(
                     stop=(g == PASSES - 1),
                 )
             if half == 1:
-                nc.scalar.activation(
-                    out=tiles["v_t"][:, h * S : (h + 1) * S], in_=tiles["v_bank"][:], func=ACT.Relu, bias=bias_col[:, h : h + 1]
-                )
+                v_t = tiles["v_t"][:, h * S : (h + 1) * S]
+                if on_vector:
+                    nc.vector.tensor_scalar(
+                        out=v_t, in0=tiles["v_bank"][:], scalar1=bias_col[:, h : h + 1], scalar2=0.0, op0=ALU.add, op1=ALU.max
+                    )
+                else:
+                    nc.scalar.activation(out=v_t, in_=tiles["v_bank"][:], func=ACT.Relu, bias=bias_col[:, h : h + 1])
 
         def values_bank(b, pair):
             tiles = batch[b]
             if pair == 0:
                 tiles["v_grouped"] = ready.tile([P, D * 2], F32, name="v_grouped", align_bytes=64)
-            bank = transpose_pairs(tiles["v_t"], S // 2, 0, pair, turn_ps)
+            bank = transpose_pairs(tiles["v_t"], S // 2, 0, pair, turn_ps, "turn")
             copy_pairs(bank, rows_of(tiles["v_grouped"], 0, pair))
 
         def quantise_values(b):
@@ -207,29 +220,53 @@ def tile_multiheadattentionlayer_pa_t_kernel(
         wv_grouped = const.tile([P, PASSES * D * 2], F32, name="wv_grouped", align_bytes=64)
         wv_codes = const.tile([P, PASSES * D], U32, name="wv_codes", align_bytes=64)
         wv_scales = const.tile([P, PASSES * D], U8, name="wv_scales", align_bytes=64)
-        for g in range(PASSES):
-            for pair in range(TILES // PAIR):
-                copy_pairs(transpose_pairs(wv_sb, DK // 2, g * (K_PASS // 2), pair, turn_ps), rows_of(wv_grouped, g, pair))
-        for g in range(PASSES):
-            quantise_pass(wv_grouped, wv_codes, wv_scales, g)
-        for part in range(4):
-            keys_bank(0, part)
-        for g in range(PASSES):
-            quantise_keys(0, g)
-        for part in range(4):
-            bank, heads = heads_bank(0, part)
-            nc.scalar.copy(out=heads, in_=bank[:])
-        bias_bank = turn_ps.tile([P, P], BF16, name="bias_bank", tag="turn")
-        nc.tensor.transpose(bias_bank[:], bias_rows[:], ident_bf[:])
         bias_col = const.tile([P, H], F32, name="bias_col")
-        nc.vector.tensor_copy(out=bias_col[:], in_=bias_bank[:, 0:H])
-        for part in range(SLOTS):
-            project_values(0, part)
-        values_bank(0, 0)
-        for part in range(4):
-            keys_bank(1, part)
-        for g in range(PASSES):
-            quantise_keys(1, g)
+
+        def head():
+            spare = [(turn_ps, "turn"), (turn_ps, "turn"), (et_ps, "et"), (et_ps, "et"), (o_ps, "o_bank"), (v_ps, "v_bank")]
+            warm_bank = score_ps.tile([P, S], F32, name="warm_bank", tag="score")
+
+            def warm(n):
+                for unused in range(n):
+                    nc.tensor.matmul(out=warm_bank[:], lhsT=zeros[:, 0:P], rhs=zeros[:], start=True, stop=True)
+
+            warm(WARM_FIRST)
+            for pair in range(TILES // PAIR):
+                for g in range(PASSES):
+                    pool, tag = spare[PASSES * pair + g]
+                    bank = transpose_pairs(wv_sb, DK // 2, g * (K_PASS // 2), pair, pool, tag)
+                    copy_pairs(bank, rows_of(wv_grouped, g, pair), on_vector=(g == 0))
+                    warm(WARM_EACH)
+            for g in range(PASSES):
+                quantise_pass(wv_grouped, wv_codes, wv_scales, g)
+            for pair in range(TILES // PAIR):
+                for g in range(PASSES):
+                    pool, tag = spare[(4 + PASSES * pair + g) % 6]
+                    keys_bank(0, g, pair, pool, tag, on_vector=(g == 0))
+                    warm(WARM_EACH)
+            for g in range(PASSES):
+                quantise_keys(0, g)
+            bias_bank = score_ps.tile([P, P], BF16, name="bias_bank", tag="score")
+            nc.tensor.transpose(bias_bank[:], bias_rows[:], ident_bf[:])
+            nc.vector.tensor_copy(out=bias_col[:], in_=bias_bank[:, 0:H])
+            for part in range(4):
+                pool, tag = spare[(2 + part) % 4]
+                bank, heads = heads_bank(0, part, pool, tag)
+                copy_out(heads, bank[:], on_vector=(part > 0))
+                if part < 3:
+                    warm(WARM_EACH)
+            for part in range(SLOTS):
+                pool, tag = ((v_ps, "v_bank"), (o_ps, "o_bank"), (score_ps, "score"), (score_ps, "score"))[part // 2]
+                project_values(0, part, pool, tag, on_vector=(part // 2 == 1))
+            for pair in range(TILES // PAIR):
+                for g in range(PASSES):
+                    pool, tag = spare[PASSES * pair + g]
+                    keys_bank(1, g, pair, pool, tag, on_vector=(g == 0))
+            values_bank(0, 0)
+            for i in range(PAIR):
+                scores(0, i)
+            for g in range(PASSES):
+                quantise_keys(1, g)
 
         steps = [(b, a, h) for b in range(B) for a in range(HALVES) for h in range(H)]
         n_steps = len(steps)
@@ -239,7 +276,7 @@ def tile_multiheadattentionlayer_pa_t_kernel(
         def scores(j, i):
             b, a, h = steps[j]
             t = PAIR * a + i
-            bank = score_ps.tile([P, S], F32, name="score_bank")
+            bank = score_ps.tile([P, S], F32, name="score_bank", tag="score")
             nc.tensor.matmul(
                 out=bank[:], lhsT=batch[b]["q_t"][:, h, t * P : (t + 1) * P], rhs=batch[b]["k_t"][:, h, :],
                 start=True, stop=True,
@@ -270,7 +307,7 @@ def tile_multiheadattentionlayer_pa_t_kernel(
                 )
 
         def transpose_e(j):
-            live[j]["et_bank"] = transpose_pairs(live[j]["e_sb"], S // 2, 0, 0, et_ps)
+            live[j]["et_bank"] = transpose_pairs(live[j]["e_sb"], S // 2, 0, 0, et_ps, "et")
 
         def copy_e(j):
             tiles = live[j]
@@ -283,7 +320,7 @@ def tile_multiheadattentionlayer_pa_t_kernel(
             e_codes = flow.tile([P, PAIR * P], U32, name="e_codes", align_bytes=64)
             e_scales = flow.tile([P, PAIR * P], U8, name="e_scales", align_bytes=64)
             nc.vector.quantize_mx(out=e_codes[:].bitcast(FP8X4), scales=e_scales[:], in_=tiles["e_grouped"][:].bitcast(BF16))
-            bank = o_ps.tile([P, PAIR, DH], F32, name="o_bank")
+            bank = o_ps.tile([P, PAIR, DH], F32, name="o_bank", tag="o_bank")
             for i in range(PAIR):
                 nc.tensor.matmul_mx(
                     out=bank[:, i, :],
@@ -327,49 +364,68 @@ def tile_multiheadattentionlayer_pa_t_kernel(
                     op0=ALU.mult, op1=ALU.add,
                 )
 
-        def layer_norm_and_store(b, a, on_vector):
-            y = y_of[b, a]["y"]
+        def statistics(b, a, i):
+            nc.vector.bn_stats(out=y_of[b, a]["stats"][:, i, :], in_=y_of[b, a]["y"][:, i, :])
+
+        def aggregate(b, a):
             mean_var = flow.tile([P, PAIR, 2], F32, name="mean_var")
             for i in range(PAIR):
                 nc.vector.bn_aggr(out=mean_var[:, i, :], in_=y_of[b, a]["stats"][:, i, :])
+            y_of[b, a]["mean_var"] = mean_var
+
+        def store(b, a, i):
+            first = (a * PAIR + i) * P
+            nc.sync.dma_start(out=out[b, first : first + P, :], in_=y_of[b, a]["y"][:, i, :])
+
+        def layer_norm(b, a):
+            y = y_of[b, a]["y"]
+            mean_var = y_of[b, a]["mean_var"]
             inv_std = flow.tile([P, PAIR], F32, name="inv_std")
-            if not on_vector:
-                var_eps = flow.tile([P, PAIR], F32, name="var_eps")
-                nc.gpsimd.tensor_scalar(
-                    out=var_eps[:], in0=mean_var[:, :, 1], scalar1=LN_EPS, scalar2=1.0, op0=ALU.add, op1=ALU.mult
-                )
-                neg_mean = flow.tile([P, PAIR], F32, name="neg_mean")
-                nc.gpsimd.tensor_scalar(
-                    out=neg_mean[:], in0=mean_var[:, :, 0], scalar1=-1.0, scalar2=0.0, op0=ALU.mult, op1=ALU.add
-                )
-                nc.gpsimd.tensor_tensor(out=inv_std[:], in0=var_eps[:], in1=neg_half[:], op=ALU.pow)
-                for i in range(PAIR):
-                    nc.gpsimd.tensor_scalar(
-                        out=y[:, i, :], in0=y[:, i, :], scalar1=neg_mean[:, i : i + 1],
-                        scalar2=inv_std[:, i : i + 1], op0=ALU.add, op1=ALU.mult,
-                    )
-                pieces = [(i, slice(first, first + LN_PIECE)) for i in range(PAIR) for first in range(0, D, LN_PIECE)]
-                for i, cols in pieces:
-                    nc.gpsimd.tensor_tensor(out=y[:, i, cols], in0=y[:, i, cols], in1=gamma_bc[:, cols], op=ALU.mult)
-                for i, cols in pieces:
-                    nc.gpsimd.tensor_tensor(out=y[:, i, cols], in0=y[:, i, cols], in1=beta_bc[:, cols], op=ALU.add)
-            else:
-                std = flow.tile([P, PAIR], F32, name="std")
-                nc.scalar.activation(out=std[:], in_=mean_var[:, :, 1], func=ACT.Sqrt, bias=eps_col[:])
-                for i in range(PAIR):
-                    nc.vector.scalar_tensor_tensor(
-                        out=y[:, i, :], in0=y[:, i, :], scalar=mean_var[:, i, 0:1], in1=gamma_bc[:],
-                        op0=ALU.subtract, op1=ALU.mult,
-                    )
-                nc.vector.reciprocal(out=inv_std[:], in_=std[:])
-                for i in range(PAIR):
-                    nc.vector.scalar_tensor_tensor(
-                        out=y[:, i, :], in0=y[:, i, :], scalar=inv_std[:, i : i + 1], in1=beta_bc[:],
-                        op0=ALU.mult, op1=ALU.add,
-                    )
+            var_eps = flow.tile([P, PAIR], F32, name="var_eps")
+            nc.gpsimd.tensor_scalar(
+                out=var_eps[:], in0=mean_var[:, :, 1], scalar1=LN_EPS, scalar2=1.0, op0=ALU.add, op1=ALU.mult
+            )
+            neg_mean = flow.tile([P, PAIR], F32, name="neg_mean")
+            nc.gpsimd.tensor_scalar(
+                out=neg_mean[:], in0=mean_var[:, :, 0], scalar1=-1.0, scalar2=0.0, op0=ALU.mult, op1=ALU.add
+            )
+            nc.gpsimd.tensor_tensor(out=inv_std[:], in0=var_eps[:], in1=neg_half[:], op=ALU.pow)
             for i in range(PAIR):
-                first = (a * PAIR + i) * P
-                nc.sync.dma_start(out=out[b, first : first + P, :], in_=y[:, i, :])
+                nc.gpsimd.tensor_scalar(
+                    out=y[:, i, :], in0=y[:, i, :], scalar1=neg_mean[:, i : i + 1],
+                    scalar2=inv_std[:, i : i + 1], op0=ALU.add, op1=ALU.mult,
+                )
+            pieces = [(i, slice(first, first + LN_PIECE)) for i in range(PAIR) for first in range(0, D, LN_PIECE)]
+            for i, cols in pieces:
+                nc.gpsimd.tensor_tensor(out=y[:, i, cols], in0=y[:, i, cols], in1=gamma_bc[:, cols], op=ALU.mult)
+            for i, cols in pieces:
+                nc.gpsimd.tensor_tensor(out=y[:, i, cols], in0=y[:, i, cols], in1=beta_bc[:, cols], op=ALU.add)
+            for i in range(PAIR):
+                store(b, a, i)
+
+        def centre(b, a):
+            y = y_of[b, a]["y"]
+            for i in range(PAIR):
+                nc.vector.scalar_tensor_tensor(
+                    out=y[:, i, :], in0=y[:, i, :], scalar=y_of[b, a]["mean_var"][:, i, 0:1], in1=gamma_bc[:],
+                    op0=ALU.subtract, op1=ALU.mult,
+                )
+
+        def deviation(b, a):
+            std = flow.tile([P, PAIR], F32, name="std")
+            nc.scalar.activation(out=std[:], in_=y_of[b, a]["mean_var"][:, :, 1], func=ACT.Sqrt, bias=eps_col[:])
+            y_of[b, a]["std"] = std
+
+        def rescale(b, a):
+            y = y_of[b, a]["y"]
+            inv_std = flow.tile([P, PAIR], F32, name="inv_std")
+            nc.vector.reciprocal(out=inv_std[:], in_=y_of[b, a]["std"][:])
+            for i in range(PAIR):
+                nc.vector.scalar_tensor_tensor(
+                    out=y[:, i, :], in0=y[:, i, :], scalar=inv_std[:, i : i + 1], in1=beta_bc[:],
+                    op0=ALU.mult, op1=ALU.add,
+                )
+                store(b, a, i)
 
         def is_step(j):
             return 0 <= j < n_steps
@@ -377,10 +433,10 @@ def tile_multiheadattentionlayer_pa_t_kernel(
         def completes_rows(j):
             return is_step(j) and steps[j][2] == H - 1
 
-        for i in range(PAIR):
-            scores(0, i)
         with tc.manual_schedule():
-            for j in range(n_steps + STATS_LAG + PAIR):
+            head()
+            last, before_last = (B - 1, HALVES - 1), (B - 1, HALVES - 2)
+            for j in range(n_steps + ATTEND_LAG):
                 b = j // SLOTS
                 slot = j % SLOTS
                 if slot == 0 and b + 3 < B:
@@ -393,7 +449,7 @@ def tile_multiheadattentionlayer_pa_t_kernel(
                 if is_step(j - COPY_LAG):
                     copy_e(j - COPY_LAG)
                 if slot < 4 and b + 2 < B:
-                    keys_bank(b + 2, slot)
+                    keys_bank(b + 2, slot // 2, slot % 2)
                 if slot >= 4 and b + 1 < B:
                     heads_ps, heads = heads_bank(b + 1, slot - 4)
                     if slot % 2 == 0:
@@ -431,12 +487,27 @@ def tile_multiheadattentionlayer_pa_t_kernel(
                     row_mask(j)
 
                 for i in range(PAIR):
-                    if completes_rows(j - STATS_LAG - i):
-                        done = y_of[steps[j - STATS_LAG - i][0], steps[j - STATS_LAG - i][1]]
-                        nc.vector.bn_stats(out=done["stats"][:, i, :], in_=done["y"][:, i, :])
+                    if completes_rows(j - STATS_LAG - i) and j < n_steps - 1:
+                        statistics(steps[j - STATS_LAG - i][0], steps[j - STATS_LAG - i][1], i)
+                if j == n_steps - 1:
+                    for i in range(PAIR):
+                        statistics(*before_last, i)
+                if j == n_steps + ATTEND_LAG - 1:
+                    rescale(*before_last)
                 if is_step(j - ATTEND_LAG):
                     add_residual(j - ATTEND_LAG)
-                if completes_rows(j - STATS_LAG - (PAIR - 1)):
-                    layer_norm_and_store(
-                        steps[j - STATS_LAG - (PAIR - 1)][0], steps[j - STATS_LAG - (PAIR - 1)][1], on_vector=j >= n_steps
-                    )
+                if completes_rows(j - STATS_LAG - (PAIR - 1)) and j < n_steps - 1:
+                    rows = (steps[j - STATS_LAG - (PAIR - 1)][0], steps[j - STATS_LAG - (PAIR - 1)][1])
+                    aggregate(*rows)
+                    layer_norm(*rows)
+                if j == n_steps - 1:
+                    aggregate(*before_last)
+                if j == n_steps:
+                    deviation(*before_last)
+                    centre(*before_last)
+            for i in range(PAIR):
+                statistics(*last, i)
+            aggregate(*last)
+            deviation(*last)
+            centre(*last)
+            rescale(*last)

@@ -23,6 +23,8 @@ HALVES = TILES // PAIR
 SLOTS = HALVES * H
 SCALE = 1.0 / DH ** 0.5
 LN_EPS = 1e-8
+SCALAR_MASKS = (3,)
+SCALAR_HEADS = (4, 5, 6, 7)
 WARM_FIRST = 6
 WARM_EACH = 1
 LN_PIECE = 256
@@ -106,6 +108,7 @@ def tile_multiheadattentionlayer_pa_t_kernel(
         nc.gpsimd.memset(neg_half[:], -0.5)
         eps_col = const.tile([P, 1], F32, name="eps_col")
         nc.gpsimd.memset(eps_col[:], LN_EPS)
+        abs_sum = const.tile([P, B * TILES], F32, name="abs_sum")
         mask01 = const.tile([P, B * TILES], F32, name="mask01")
 
         def transpose_pairs(rows_sb, row_words, first, pair, pool, tag):
@@ -166,7 +169,8 @@ def tile_multiheadattentionlayer_pa_t_kernel(
                     nc.tensor.transpose(
                         bank[:, hh, t * P : (t + 1) * P], rows_sb[:, t, h * DH : (h + 1) * DH], ident_bf[:]
                     )
-            return bank, heads_t[:, first_head : first_head + PAIR, :]
+            words_out = heads_t[:].rearrange("p h s -> p (h s)")[:, first_head * S : (first_head + PAIR) * S].bitcast(F32)
+            return bank[:].rearrange("p h s -> p (h s)").bitcast(F32), words_out
 
         def project_values(b, part, pool=v_ps, tag="v_bank", on_vector=False):
             tiles = batch[b]
@@ -211,11 +215,22 @@ def tile_multiheadattentionlayer_pa_t_kernel(
 
         def row_mask(b):
             for t in range(TILES):
-                unread = flow.tile([P, D], BF16, name="unread")
-                nc.vector.tensor_scalar(
-                    out=unread[:], in0=x_sb[:, b, t, :], scalar1=0.0, scalar2=None, op0=ALU.not_equal, op1=ALU.max,
-                    accum_out=mask01[:, b * TILES + t : b * TILES + t + 1],
-                )
+                if t in SCALAR_MASKS:
+                    unread = flow.tile([P, D], BF16, name="unread_s")
+                    nc.scalar.activation(
+                        out=unread[:], in_=x_sb[:, b, t, :], func=ACT.Abs, accum_out=abs_sum[:, b * TILES + t : b * TILES + t + 1]
+                    )
+                else:
+                    unread = flow.tile([P, D], BF16, name="unread")
+                    nc.vector.tensor_scalar(
+                        out=unread[:], in0=x_sb[:, b, t, :], scalar1=0.0, scalar2=None, op0=ALU.not_equal, op1=ALU.max,
+                        accum_out=mask01[:, b * TILES + t : b * TILES + t + 1],
+                    )
+
+        def compare_sums(b):
+            for t in SCALAR_MASKS:
+                col = slice(b * TILES + t, b * TILES + t + 1)
+                nc.vector.tensor_scalar(out=mask01[:, col], in0=abs_sum[:, col], scalar1=0.0, scalar2=None, op0=ALU.is_gt)
 
         wv_grouped = const.tile([P, PASSES * D * 2], F32, name="wv_grouped", align_bytes=64)
         wv_codes = const.tile([P, PASSES * D], U32, name="wv_codes", align_bytes=64)
@@ -252,7 +267,7 @@ def tile_multiheadattentionlayer_pa_t_kernel(
             for part in range(4):
                 pool, tag = spare[(2 + part) % 4]
                 bank, heads = heads_bank(0, part, pool, tag)
-                copy_out(heads, bank[:], on_vector=(part > 0))
+                copy_out(heads, bank, on_vector=(part % 2 == 1))
                 if part < 3:
                     warm(WARM_EACH)
             for part in range(SLOTS):
@@ -435,6 +450,7 @@ def tile_multiheadattentionlayer_pa_t_kernel(
 
         with tc.manual_schedule():
             head()
+            tail = n_steps - H + ATTEND_LAG
             last, before_last = (B - 1, HALVES - 1), (B - 1, HALVES - 2)
             for j in range(n_steps + ATTEND_LAG):
                 b = j // SLOTS
@@ -452,8 +468,8 @@ def tile_multiheadattentionlayer_pa_t_kernel(
                     keys_bank(b + 2, slot // 2, slot % 2)
                 if slot >= 4 and b + 1 < B:
                     heads_ps, heads = heads_bank(b + 1, slot - 4)
-                    if slot % 2 == 0:
-                        nc.scalar.copy(out=heads, in_=heads_ps[:])
+                    if slot in SCALAR_HEADS:
+                        nc.scalar.copy(out=heads, in_=heads_ps)
                 if slot == 5 and b + 1 < B:
                     values_bank(b + 1, 0)
                 if slot == 0 and b < B:
@@ -477,32 +493,34 @@ def tile_multiheadattentionlayer_pa_t_kernel(
                 if is_step(j - EXP_LAG):
                     transpose_e(j - EXP_LAG)
 
-                if slot >= 4 and slot % 2 == 1 and b + 1 < B:
-                    nc.vector.tensor_copy(out=heads, in_=heads_ps[:])
+                if slot >= 4 and slot not in SCALAR_HEADS and b + 1 < B:
+                    nc.vector.tensor_copy(out=heads, in_=heads_ps)
                 if slot == 1 and b < B:
                     quantise_values(b)
                 if slot in (2, 4) and b + 2 < B:
                     quantise_keys(b + 2, (slot - 2) // 2)
                 if j < B:
                     row_mask(j)
+                if 0 < j <= B:
+                    compare_sums(j - 1)
 
                 for i in range(PAIR):
-                    if completes_rows(j - STATS_LAG - i) and j < n_steps - 1:
+                    if completes_rows(j - STATS_LAG - i) and j < tail:
                         statistics(steps[j - STATS_LAG - i][0], steps[j - STATS_LAG - i][1], i)
-                if j == n_steps - 1:
+                if j == tail:
                     for i in range(PAIR):
                         statistics(*before_last, i)
-                if j == n_steps + ATTEND_LAG - 1:
+                if j == tail + 3:
                     rescale(*before_last)
                 if is_step(j - ATTEND_LAG):
                     add_residual(j - ATTEND_LAG)
-                if completes_rows(j - STATS_LAG - (PAIR - 1)) and j < n_steps - 1:
+                if completes_rows(j - STATS_LAG - (PAIR - 1)) and j < tail:
                     rows = (steps[j - STATS_LAG - (PAIR - 1)][0], steps[j - STATS_LAG - (PAIR - 1)][1])
                     aggregate(*rows)
                     layer_norm(*rows)
-                if j == n_steps - 1:
+                if j == tail:
                     aggregate(*before_last)
-                if j == n_steps:
+                if j == tail + 1:
                     deviation(*before_last)
                     centre(*before_last)
             for i in range(PAIR):

@@ -23,15 +23,15 @@ HALVES = TILES // PAIR
 SLOTS = HALVES * H
 SCALE = 1.0 / DH ** 0.5
 LN_EPS = 1e-8
-SCALAR_MASKS = (3,)
-SCALAR_HEADS = (4, 5, 6, 7)
+SCALAR_MASKS = ()
+SCALAR_HEADS = (4, 6)
 WARM_FIRST = 6
 WARM_EACH = 1
 LN_PIECE = 256
 EXP_LAG = 1
 COPY_LAG = 2
-ATTEND_LAG = 3
-STATS_LAG = 4
+ATTEND_LAG = 4
+STATS_LAG = 5
 
 FLOPS = 2 * B * S * DK * D + 2 * 2 * B * H * S * S * DH
 
@@ -270,6 +270,10 @@ def tile_multiheadattentionlayer_pa_t_kernel(
                 copy_out(heads, bank, on_vector=(part % 2 == 1))
                 if part < 3:
                     warm(WARM_EACH)
+            for i in range(PAIR):
+                scores(0, i)
+            for i in range(PAIR):
+                row_max(0, i)
             for part in range(SLOTS):
                 pool, tag = ((v_ps, "v_bank"), (o_ps, "o_bank"), (score_ps, "score"), (score_ps, "score"))[part // 2]
                 project_values(0, part, pool, tag, on_vector=(part // 2 == 1))
@@ -278,8 +282,6 @@ def tile_multiheadattentionlayer_pa_t_kernel(
                     pool, tag = spare[PASSES * pair + g]
                     keys_bank(1, g, pair, pool, tag, on_vector=(g == 0))
             values_bank(0, 0)
-            for i in range(PAIR):
-                scores(0, i)
             for g in range(PASSES):
                 quantise_keys(1, g)
 
@@ -325,22 +327,32 @@ def tile_multiheadattentionlayer_pa_t_kernel(
             live[j]["et_bank"] = transpose_pairs(live[j]["e_sb"], S // 2, 0, 0, et_ps, "et")
 
         def copy_e(j):
+            if j % 2 == 0:
+                live[j]["e_grouped"] = flow.tile([P, 2 * PAIR * P * 2], F32, name="e_grouped", align_bytes=64)
+            copy_pairs(live[j]["et_bank"], rows_of(live[j - j % 2]["e_grouped"], 0, j % 2))
+
+        def quantise_e(j):
             tiles = live[j]
-            tiles["e_grouped"] = flow.tile([P, PAIR * P * 2], F32, name="e_grouped", align_bytes=64)
-            copy_pairs(tiles["et_bank"], rows_of(tiles["e_grouped"], 0, 0))
+            tiles["e_codes"] = flow.tile([P, 2 * PAIR * P], U32, name="e_codes", align_bytes=64)
+            tiles["e_scales"] = flow.tile([P, 2 * PAIR * P], U8, name="e_scales", align_bytes=64)
+            nc.vector.quantize_mx(
+                out=tiles["e_codes"][:].bitcast(FP8X4), scales=tiles["e_scales"][:], in_=tiles["e_grouped"][:].bitcast(BF16)
+            )
 
         def e_times_v(j):
             b, a, h = steps[j]
             tiles = live[j]
-            e_codes = flow.tile([P, PAIR * P], U32, name="e_codes", align_bytes=64)
-            e_scales = flow.tile([P, PAIR * P], U8, name="e_scales", align_bytes=64)
-            nc.vector.quantize_mx(out=e_codes[:].bitcast(FP8X4), scales=e_scales[:], in_=tiles["e_grouped"][:].bitcast(BF16))
-            bank = o_ps.tile([P, PAIR, DH], F32, name="o_bank", tag="o_bank")
+            both = live[j - j % 2]
+            if j == n_steps - 1:
+                bank = v_ps.tile([P, PAIR, DH], F32, name="o_bank", tag="v_bank")
+            else:
+                bank = o_ps.tile([P, PAIR, DH], F32, name="o_bank", tag="o_bank")
             for i in range(PAIR):
+                rows = slice((PAIR * (j % 2) + i) * P, (PAIR * (j % 2) + i + 1) * P)
                 nc.tensor.matmul_mx(
                     out=bank[:, i, :],
-                    lhsT=e_codes[:, i * P : (i + 1) * P].bitcast(FP8X4),
-                    lhsT_scale=e_scales[:, i * P : (i + 1) * P],
+                    lhsT=both["e_codes"][:, rows].bitcast(FP8X4),
+                    lhsT_scale=both["e_scales"][:, rows],
                     rhs=batch[b]["v_codes"][:, h * DH : (h + 1) * DH].bitcast(FP8X4),
                     rhs_scale=batch[b]["v_scales"][:, h * DH : (h + 1) * DH],
                     start=True,
@@ -452,7 +464,7 @@ def tile_multiheadattentionlayer_pa_t_kernel(
             head()
             tail = n_steps - H + ATTEND_LAG
             last, before_last = (B - 1, HALVES - 1), (B - 1, HALVES - 2)
-            for j in range(n_steps + ATTEND_LAG):
+            for j in range(n_steps + ATTEND_LAG - 1):
                 b = j // SLOTS
                 slot = j % SLOTS
                 if slot == 0 and b + 3 < B:
@@ -475,30 +487,32 @@ def tile_multiheadattentionlayer_pa_t_kernel(
                 if slot == 0 and b < B:
                     values_bank(b, 1)
 
+                if is_step(j - ATTEND_LAG) and (j - ATTEND_LAG) % 2 == 0:
+                    apply_mask(j - ATTEND_LAG)
+                    quantise_e(j - ATTEND_LAG)
+                if j == n_steps + ATTEND_LAG - 2:
+                    centre(*before_last)
+                if slot == 2 and b < B:
+                    quantise_values(b)
+                if slot in (4, 6) and b + 2 < B:
+                    quantise_keys(b + 2, (slot - 4) // 2)
                 if is_step(j - ATTEND_LAG):
                     e_times_v(j - ATTEND_LAG)
                 if b + 1 < B:
                     project_values(b + 1, slot)
 
                 for i in range(PAIR):
-                    if is_step(j):
+                    if is_step(j) and j > 0:
                         row_max(j, i)
                     if is_step(j + 1):
                         scores(j + 1, i)
-                    if is_step(j - ATTEND_LAG) and (j - ATTEND_LAG) % 2 == 0:
-                        if i == 0:
-                            invert_row_sums(j - ATTEND_LAG)
-                        else:
-                            apply_mask(j - ATTEND_LAG)
+                    if i == 0 and is_step(j + 1 - ATTEND_LAG) and (j + 1 - ATTEND_LAG) % 2 == 0:
+                        invert_row_sums(j + 1 - ATTEND_LAG)
                 if is_step(j - EXP_LAG):
                     transpose_e(j - EXP_LAG)
 
                 if slot >= 4 and slot not in SCALAR_HEADS and b + 1 < B:
                     nc.vector.tensor_copy(out=heads, in_=heads_ps)
-                if slot == 1 and b < B:
-                    quantise_values(b)
-                if slot in (2, 4) and b + 2 < B:
-                    quantise_keys(b + 2, (slot - 2) // 2)
                 if j < B:
                     row_mask(j)
                 if 0 < j <= B:
@@ -510,8 +524,6 @@ def tile_multiheadattentionlayer_pa_t_kernel(
                 if j == tail:
                     for i in range(PAIR):
                         statistics(*before_last, i)
-                if j == tail + 3:
-                    rescale(*before_last)
                 if is_step(j - ATTEND_LAG):
                     add_residual(j - ATTEND_LAG)
                 if completes_rows(j - STATS_LAG - (PAIR - 1)) and j < tail:
@@ -522,9 +534,11 @@ def tile_multiheadattentionlayer_pa_t_kernel(
                     aggregate(*before_last)
                 if j == tail + 1:
                     deviation(*before_last)
-                    centre(*before_last)
+            e_times_v(n_steps - 1)
+            add_residual(n_steps - 1)
             for i in range(PAIR):
                 statistics(*last, i)
+            rescale(*before_last)
             aggregate(*last)
             deviation(*last)
             centre(*last)

@@ -23,8 +23,8 @@ HALVES = TILES // PAIR
 SLOTS = HALVES * H
 SCALE = 1.0 / DH ** 0.5
 LN_EPS = 1e-8
-SCALAR_MASKS = ()
-SCALAR_HEADS = (4, 6)
+SCALAR_MASKS = (3,)
+SCALAR_HEADS = (4, 5, 6, 7)
 WARM_FIRST = 6
 WARM_EACH = 1
 LN_PIECE = 256

@@ -24,7 +24,7 @@ SLOTS = HALVES * H
 SCALE = 1.0 / DH ** 0.5
 LN_EPS = 1e-8
 SCALAR_MASKS = (3,)
-SCALAR_HEADS = (4, 5, 6, 7)
+SCALAR_HEADS = (4, 6, 7)
 WARM_FIRST = 6
 WARM_EACH = 1
 LN_PIECE = 256
@@ -89,9 +89,10 @@ def tile_multiheadattentionlayer_pa_t_kernel(
         nc.sync.dma_start(out=bias_rows[0:H, :], in_=bv.rearrange("(h c) -> h c", h=H))
         load_heads(0)
         load_keys(1)
-        for b in range(B // 2):
-            load_queries(b)
+        load_queries(0)
         load_keys(2)
+        for b in range(1, B // 2):
+            load_queries(b)
         load_heads(1)
         for b in range(B // 2, B):
             load_queries(b)
@@ -251,14 +252,14 @@ def tile_multiheadattentionlayer_pa_t_kernel(
                     pool, tag = spare[PASSES * pair + g]
                     bank = transpose_pairs(wv_sb, DK // 2, g * (K_PASS // 2), pair, pool, tag)
                     copy_pairs(bank, rows_of(wv_grouped, g, pair), on_vector=(g == 0))
-                    warm(WARM_EACH)
+                    warm(g)
             for g in range(PASSES):
                 quantise_pass(wv_grouped, wv_codes, wv_scales, g)
             for pair in range(TILES // PAIR):
                 for g in range(PASSES):
                     pool, tag = spare[(4 + PASSES * pair + g) % 6]
                     keys_bank(0, g, pair, pool, tag, on_vector=(g == 0))
-                    warm(WARM_EACH)
+                    warm(g)
             for g in range(PASSES):
                 quantise_keys(0, g)
             bias_bank = score_ps.tile([P, P], BF16, name="bias_bank", tag="score")
@@ -275,11 +276,14 @@ def tile_multiheadattentionlayer_pa_t_kernel(
             for i in range(PAIR):
                 row_max(0, i)
             for part in range(SLOTS):
-                pool, tag = ((v_ps, "v_bank"), (o_ps, "o_bank"), (score_ps, "score"), (score_ps, "score"))[part // 2]
+                pool, tag = ((v_ps, "v_bank"), (o_ps, "o_bank"), (turn_ps, "turn"), (turn_ps, "turn"))[part // 2]
                 project_values(0, part, pool, tag, on_vector=(part // 2 == 1))
+            for i in range(PAIR):
+                scores(1, i)
+            row_mask(0)
             for pair in range(TILES // PAIR):
                 for g in range(PASSES):
-                    pool, tag = spare[PASSES * pair + g]
+                    pool, tag = spare[2 + PASSES * pair + g]
                     keys_bank(1, g, pair, pool, tag, on_vector=(g == 0))
             values_bank(0, 0)
             for g in range(PASSES):
@@ -504,7 +508,7 @@ def tile_multiheadattentionlayer_pa_t_kernel(
                 for i in range(PAIR):
                     if is_step(j) and j > 0:
                         row_max(j, i)
-                    if is_step(j + 1):
+                    if is_step(j + 1) and j > 0:
                         scores(j + 1, i)
                     if i == 0 and is_step(j + 1 - ATTEND_LAG) and (j + 1 - ATTEND_LAG) % 2 == 0:
                         invert_row_sums(j + 1 - ATTEND_LAG)
@@ -513,7 +517,7 @@ def tile_multiheadattentionlayer_pa_t_kernel(
 
                 if slot >= 4 and slot not in SCALAR_HEADS and b + 1 < B:
                     nc.vector.tensor_copy(out=heads, in_=heads_ps)
-                if j < B:
+                if 0 < j < B:
                     row_mask(j)
                 if 0 < j <= B:
                     compare_sums(j - 1)

@@ -148,12 +148,14 @@ def tile_multiheadattentionlayer_pa_t_kernel(
             bank = transpose_pairs(tiles["keys_sb"], DK // 2, g * (K_PASS // 2), pair, pool, tag)
             copy_pairs(bank, rows_of(tiles["keys_grouped"], g, pair), on_vector)
 
-        def quantise_keys(b, g):
+        def quantise_keys(b):
             tiles = batch[b]
-            if g == 0:
-                tiles["keys_codes"] = ready.tile([P, PASSES * S], U32, name="keys_codes", align_bytes=64)
-                tiles["keys_scales"] = ready.tile([P, PASSES * S], U8, name="keys_scales", align_bytes=64)
-            quantise_pass(tiles["keys_grouped"], tiles["keys_codes"], tiles["keys_scales"], g)
+            tiles["keys_codes"] = ready.tile([P, PASSES * S], U32, name="keys_codes", align_bytes=64)
+            tiles["keys_scales"] = ready.tile([P, PASSES * S], U8, name="keys_scales", align_bytes=64)
+            nc.vector.quantize_mx(
+                out=tiles["keys_codes"][:].bitcast(FP8X4), scales=tiles["keys_scales"][:],
+                in_=tiles["keys_grouped"][:].bitcast(BF16),
+            )
 
         def heads_bank(b, part, pool=turn_ps, tag="turn"):
             tiles = batch[b]
@@ -260,8 +262,7 @@ def tile_multiheadattentionlayer_pa_t_kernel(
                     pool, tag = spare[(4 + PASSES * pair + g) % 6]
                     keys_bank(0, g, pair, pool, tag, on_vector=(g == 0))
                     warm(g)
-            for g in range(PASSES):
-                quantise_keys(0, g)
+            quantise_keys(0)
             bias_bank = score_ps.tile([P, P], BF16, name="bias_bank", tag="score")
             nc.tensor.transpose(bias_bank[:], bias_rows[:], ident_bf[:])
             nc.vector.tensor_copy(out=bias_col[:], in_=bias_bank[:, 0:H])
@@ -286,8 +287,7 @@ def tile_multiheadattentionlayer_pa_t_kernel(
                     pool, tag = spare[2 + PASSES * pair + g]
                     keys_bank(1, g, pair, pool, tag, on_vector=(g == 0))
             values_bank(0, 0)
-            for g in range(PASSES):
-                quantise_keys(1, g)
+            quantise_keys(1)
 
         steps = [(b, a, h) for b in range(B) for a in range(HALVES) for h in range(H)]
         n_steps = len(steps)
@@ -486,7 +486,7 @@ def tile_multiheadattentionlayer_pa_t_kernel(
                     heads_ps, heads = heads_bank(b + 1, slot - 4)
                     if slot in SCALAR_HEADS:
                         nc.scalar.copy(out=heads, in_=heads_ps)
-                if slot == 5 and b + 1 < B:
+                if slot == 6 and b + 1 < B:
                     values_bank(b + 1, 0)
                 if slot == 0 and b < B:
                     values_bank(b, 1)
@@ -496,10 +496,10 @@ def tile_multiheadattentionlayer_pa_t_kernel(
                     quantise_e(j - ATTEND_LAG)
                 if j == n_steps + ATTEND_LAG - 2:
                     centre(*before_last)
-                if slot == 2 and b < B:
+                if slot == 3 and b < B:
                     quantise_values(b)
-                if slot in (4, 6) and b + 2 < B:
-                    quantise_keys(b + 2, (slot - 4) // 2)
+                if slot == 7 and b + 2 < B:
+                    quantise_keys(b + 2)
                 if is_step(j - ATTEND_LAG):
                     e_times_v(j - ATTEND_LAG)
                 if b + 1 < B:

from contextlib import ExitStack

import concourse.mybir as mybir
from concourse.masks import make_identity

F32 = mybir.dt.float32
BF16 = mybir.dt.bfloat16
U32 = mybir.dt.uint32
U8 = mybir.dt.uint8
FP8X4 = mybir.dt.float8_e4m3fn_x4
ALU = mybir.AluOpType
ACT = mybir.ActivationFunctionType

B, S, D, DK, H = 8, 512, 512, 1024, 4
DH = D // H
P = 128
PACK = 4
K_PASS = P * PACK
PASSES = DK // K_PASS
TILES = S // P
PAIR = 2
HALVES = TILES // PAIR
SLOTS = HALVES * H
SCALE = 1.0 / DH ** 0.5
LN_EPS = 1e-8
SCALAR_MASKS = (3,)
SCALAR_HEADS = (4, 6, 7)
WARM_FIRST = 6
WARM_EACH = 1
LN_PIECE = 256
EXP_LAG = 1
COPY_LAG = 2
ATTEND_LAG = 4
STATS_LAG = 5

FLOPS = 2 * B * S * DK * D + 2 * 2 * B * H * S * S * DH


def tile_multiheadattentionlayer_pa_t_kernel(
    tc, q_relu, k_relu, keys, Wv, bv, queries, ln_gamma, ln_beta, out
):
    nc = tc.nc
    with ExitStack() as ctx:
        const = ctx.enter_context(tc.tile_pool(name="const", bufs=1))
        loads = ctx.enter_context(tc.tile_pool(name="loads", bufs=2))
        ready = ctx.enter_context(tc.tile_pool(name="ready", bufs=2))
        flow = ctx.enter_context(tc.tile_pool(name="flow", bufs=4))
        score_ps = ctx.enter_context(tc.psum_pool(name="score_ps", bufs=2))
        et_ps = ctx.enter_context(tc.psum_pool(name="et_ps", bufs=2))
        o_ps = ctx.enter_context(tc.psum_pool(name="o_ps", bufs=1))
        v_ps = ctx.enter_context(tc.psum_pool(name="v_ps", bufs=1))
        turn_ps = ctx.enter_context(tc.psum_pool(name="turn_ps", bufs=2))

        batch = {b: {} for b in range(B)}

        def load_row_pairs(rows_sb, rows):
            for pair in range(TILES // PAIR):
                tiles = slice(PAIR * pair, PAIR * (pair + 1))
                nc.sync.dma_start(
                    out=rows_sb[:].rearrange("p (t k) -> p t k", t=TILES)[:, tiles, :],
                    in_=rows.rearrange("(t p) k -> p t k", p=P)[:, tiles, :],
                )

        def load_keys(b):
            keys_sb = loads.tile([P, TILES * DK], BF16, name="keys_sb", bufs=3)
            load_row_pairs(keys_sb, keys[b])
            batch[b]["keys_sb"] = keys_sb

        def load_heads(b):
            q_sb = loads.tile([P, TILES, D], BF16, name="q_sb")
            nc.sync.dma_start(out=q_sb[:], in_=q_relu[b].rearrange("(t p) d -> p t d", p=P))
            k_sb = loads.tile([P, TILES, D], BF16, name="k_sb")
            nc.sync.dma_start(out=k_sb[:], in_=k_relu[b].rearrange("(t p) d -> p t d", p=P))
            batch[b]["q_sb"] = q_sb
            batch[b]["k_sb"] = k_sb

        x_sb = const.tile([P, B, TILES, D], BF16, name="x_sb")

        def load_queries(b):
            nc.sync.dma_start(out=x_sb[:, b], in_=queries[b].rearrange("(t p) d -> p t d", p=P))

        zeros = const.tile([P, S], BF16, name="zeros")
        nc.vector.memset(zeros[:], 0.0)
        bias_rows = const.tile([P, P], BF16, name="bias_rows")
        nc.vector.memset(bias_rows[:], 0.0)
        wv_sb = const.tile([P, TILES * DK], BF16, name="wv_sb")
        load_row_pairs(wv_sb, Wv)
        load_keys(0)
        nc.sync.dma_start(out=bias_rows[0:H, :], in_=bv.rearrange("(h c) -> h c", h=H))
        load_heads(0)
        load_keys(1)
        load_queries(0)
        load_keys(2)
        for b in range(1, B // 2):
            load_queries(b)
        load_heads(1)
        for b in range(B // 2, B):
            load_queries(b)
        gamma_bc = const.tile([P, D], BF16, name="gamma_bc")
        nc.sync.dma_start(out=gamma_bc[:], in_=ln_gamma.partition_broadcast(P))
        beta_bc = const.tile([P, D], BF16, name="beta_bc")
        nc.sync.dma_start(out=beta_bc[:], in_=ln_beta.partition_broadcast(P))

        ident_bf = const.tile([P, P], BF16, name="ident_bf")
        make_identity(nc, ident_bf[:])
        ident_f32 = const.tile([P, P], F32, name="ident_f32")
        make_identity(nc, ident_f32[:])
        neg_half = const.tile([P, PAIR], F32, name="neg_half")
        nc.gpsimd.memset(neg_half[:], -0.5)
        eps_col = const.tile([P, 1], F32, name="eps_col")
        nc.gpsimd.memset(eps_col[:], LN_EPS)
        abs_sum = const.tile([P, B * TILES], F32, name="abs_sum")
        mask01 = const.tile([P, B * TILES], F32, name="mask01")

        def transpose_pairs(rows_sb, row_words, first, pair, pool, tag):
            words = rows_sb[:].bitcast(F32)
            bank = pool.tile([P, 2, PAIR * P], F32, name="pairs_bank", tag=tag)
            for u in range(2):
                for r in range(PAIR):
                    col = (PAIR * pair + r) * row_words + first + u * P
                    nc.tensor.transpose(bank[:, u, r * P : (r + 1) * P], words[:, col : col + P], ident_f32[:])
            return bank

        def copy_out(out, in_, on_vector):
            if on_vector:
                nc.vector.tensor_copy(out=out, in_=in_)
            else:
                nc.scalar.copy(out=out, in_=in_)

        def copy_pairs(bank, grouped_rows, on_vector=False):
            copy_out(grouped_rows, bank[:].rearrange("q u s -> q s u"), on_vector)

        def quantise_pass(grouped, codes, scales, g):
            nc.vector.quantize_mx(
                out=codes[:, g * S : (g + 1) * S].bitcast(FP8X4),
                scales=scales[:, g * S : (g + 1) * S],
                in_=grouped[:].bitcast(BF16)[:, g * S * PACK : (g + 1) * S * PACK],
            )

        def rows_of(grouped, g, pair):
            first = (g * TILES + pair * PAIR) * P * 2
            return grouped[:, first : first + PAIR * P * 2].rearrange("q (s u) -> q s u", u=2)

        def keys_bank(b, g, pair, pool=turn_ps, tag="turn", on_vector=False):
            tiles = batch[b]
            if "keys_grouped" not in tiles:
                tiles["keys_grouped"] = ready.tile([P, PASSES * S * 2], F32, name="keys_grouped", align_bytes=64)
            bank = transpose_pairs(tiles["keys_sb"], DK // 2, g * (K_PASS // 2), pair, pool, tag)
            copy_pairs(bank, rows_of(tiles["keys_grouped"], g, pair), on_vector)

        def quantise_keys(b):
            tiles = batch[b]
            tiles["keys_codes"] = ready.tile([P, PASSES * S], U32, name="keys_codes", align_bytes=64)
            tiles["keys_scales"] = ready.tile([P, PASSES * S], U8, name="keys_scales", align_bytes=64)
            nc.vector.quantize_mx(
                out=tiles["keys_codes"][:].bitcast(FP8X4), scales=tiles["keys_scales"][:],
                in_=tiles["keys_grouped"][:].bitcast(BF16),
            )

        def heads_bank(b, part, pool=turn_ps, tag="turn"):
            tiles = batch[b]
            if part == 0:
                tiles["q_t"] = ready.tile([P, H, S], BF16, name="q_t")
                tiles["k_t"] = ready.tile([P, H, S], BF16, name="k_t")
            rows_sb = tiles["q_sb"] if part % 2 == 0 else tiles["k_sb"]
            heads_t = tiles["q_t"] if part % 2 == 0 else tiles["k_t"]
            first_head = PAIR * (part // 2)
            bank = pool.tile([P, PAIR, S], BF16, name="heads_bank", tag=tag)
            for hh in range(PAIR):
                h = first_head + hh
                for t in range(TILES):
                    nc.tensor.transpose(
                        bank[:, hh, t * P : (t + 1) * P], rows_sb[:, t, h * DH : (h + 1) * DH], ident_bf[:]
                    )
            words_out = heads_t[:].rearrange("p h s -> p (h s)")[:, first_head * S : (first_head + PAIR) * S].bitcast(F32)
            return bank[:].rearrange("p h s -> p (h s)").bitcast(F32), words_out

        def project_values(b, part, pool=v_ps, tag="v_bank", on_vector=False):
            tiles = batch[b]
            h, half = part // 2, part % 2
            if part == 0:
                tiles["v_t"] = ready.tile([P, H * S], BF16, name="v_t")
            if half == 0:
                tiles["v_bank"] = pool.tile([P, S], F32, name="v_bank", tag=tag)
            for g in range(PASSES):
                out_cols = slice(g * D + h * DH, g * D + (h + 1) * DH)
                key_cols = slice(g * S + half * (S // 2), g * S + (half + 1) * (S // 2))
                nc.tensor.matmul_mx(
                    out=tiles["v_bank"][:, half * (S // 2) : (half + 1) * (S // 2)],
                    lhsT=wv_codes[:, out_cols].bitcast(FP8X4),
                    lhsT_scale=wv_scales[:, out_cols],
                    rhs=tiles["keys_codes"][:, key_cols].bitcast(FP8X4),
                    rhs_scale=tiles["keys_scales"][:, key_cols],
                    start=(g == 0),
                    stop=(g == PASSES - 1),
                )
            if half == 1:
                v_t = tiles["v_t"][:, h * S : (h + 1) * S]
                if on_vector:
                    nc.vector.tensor_scalar(
                        out=v_t, in0=tiles["v_bank"][:], scalar1=bias_col[:, h : h + 1], scalar2=0.0, op0=ALU.add, op1=ALU.max
                    )
                else:
                    nc.scalar.activation(out=v_t, in_=tiles["v_bank"][:], func=ACT.Relu, bias=bias_col[:, h : h + 1])

        def values_bank(b, pair):
            tiles = batch[b]
            if pair == 0:
                tiles["v_grouped"] = ready.tile([P, D * 2], F32, name="v_grouped", align_bytes=64)
            bank = transpose_pairs(tiles["v_t"], S // 2, 0, pair, turn_ps, "turn")
            copy_pairs(bank, rows_of(tiles["v_grouped"], 0, pair))

        def quantise_values(b):
            tiles = batch[b]
            tiles["v_codes"] = ready.tile([P, D], U32, name="v_codes", align_bytes=64)
            tiles["v_scales"] = ready.tile([P, D], U8, name="v_scales", align_bytes=64)
            quantise_pass(tiles["v_grouped"], tiles["v_codes"], tiles["v_scales"], 0)

        def row_mask(b):
            for t in range(TILES):
                if t in SCALAR_MASKS:
                    unread = flow.tile([P, D], BF16, name="unread_s")
                    nc.scalar.activation(
                        out=unread[:], in_=x_sb[:, b, t, :], func=ACT.Abs, accum_out=abs_sum[:, b * TILES + t : b * TILES + t + 1]
                    )
                else:
                    unread = flow.tile([P, D], BF16, name="unread")
                    nc.vector.tensor_scalar(
                        out=unread[:], in0=x_sb[:, b, t, :], scalar1=0.0, scalar2=None, op0=ALU.not_equal, op1=ALU.max,
                        accum_out=mask01[:, b * TILES + t : b * TILES + t + 1],
                    )

        def compare_sums(b):
            for t in SCALAR_MASKS:
                col = slice(b * TILES + t, b * TILES + t + 1)
                nc.vector.tensor_scalar(out=mask01[:, col], in0=abs_sum[:, col], scalar1=0.0, scalar2=None, op0=ALU.is_gt)

        wv_grouped = const.tile([P, PASSES * D * 2], F32, name="wv_grouped", align_bytes=64)
        wv_codes = const.tile([P, PASSES * D], U32, name="wv_codes", align_bytes=64)
        wv_scales = const.tile([P, PASSES * D], U8, name="wv_scales", align_bytes=64)
        bias_col = const.tile([P, H], F32, name="bias_col")

        def head():
            spare = [(turn_ps, "turn"), (turn_ps, "turn"), (et_ps, "et"), (et_ps, "et"), (o_ps, "o_bank"), (v_ps, "v_bank")]
            warm_bank = score_ps.tile([P, S], F32, name="warm_bank", tag="score")

            def warm(n):
                for unused in range(n):
                    nc.tensor.matmul(out=warm_bank[:], lhsT=zeros[:, 0:P], rhs=zeros[:], start=True, stop=True)

            warm(WARM_FIRST)
            for pair in range(TILES // PAIR):
                for g in range(PASSES):
                    pool, tag = spare[PASSES * pair + g]
                    bank = transpose_pairs(wv_sb, DK // 2, g * (K_PASS // 2), pair, pool, tag)
                    copy_pairs(bank, rows_of(wv_grouped, g, pair), on_vector=(g == 0))
                    warm(g)
            for g in range(PASSES):
                quantise_pass(wv_grouped, wv_codes, wv_scales, g)
            for pair in range(TILES // PAIR):
                for g in range(PASSES):
                    pool, tag = spare[(4 + PASSES * pair + g) % 6]
                    keys_bank(0, g, pair, pool, tag, on_vector=(g == 0))
                    warm(g)
            quantise_keys(0)
            bias_bank = score_ps.tile([P, P], BF16, name="bias_bank", tag="score")
            nc.tensor.transpose(bias_bank[:], bias_rows[:], ident_bf[:])
            nc.vector.tensor_copy(out=bias_col[:], in_=bias_bank[:, 0:H])
            for part in range(4):
                pool, tag = spare[(2 + part) % 4]
                bank, heads = heads_bank(0, part, pool, tag)
                copy_out(heads, bank, on_vector=(part % 2 == 1))
                if part < 3:
                    warm(WARM_EACH)
            for i in range(PAIR):
                scores(0, i)
            for i in range(PAIR):
                row_max(0, i)
            for part in range(SLOTS):
                pool, tag = ((v_ps, "v_bank"), (o_ps, "o_bank"), (turn_ps, "turn"), (turn_ps, "turn"))[part // 2]
                project_values(0, part, pool, tag, on_vector=(part // 2 == 1))
            for i in range(PAIR):
                scores(1, i)
            row_mask(0)
            for pair in range(TILES // PAIR):
                for g in range(PASSES):
                    pool, tag = spare[2 + PASSES * pair + g]
                    keys_bank(1, g, pair, pool, tag, on_vector=(g == 0))
            values_bank(0, 0)
            quantise_keys(1)

        steps = [(b, a, h) for b in range(B) for a in range(HALVES) for h in range(H)]
        n_steps = len(steps)
        live = {}
        y_of = {}

        def scores(j, i):
            b, a, h = steps[j]
            t = PAIR * a + i
            bank = score_ps.tile([P, S], F32, name="score_bank", tag="score")
            nc.tensor.matmul(
                out=bank[:], lhsT=batch[b]["q_t"][:, h, t * P : (t + 1) * P], rhs=batch[b]["k_t"][:, h, :],
                start=True, stop=True,
            )
            if i == 0:
                live[j] = {"neg_max": flow.tile([P, PAIR], F32, name="neg_max")}
            live[j]["score_bank", i] = bank

        def row_max(j, i):
            tiles = live[j]
            tiles["neg_s", i] = flow.tile([P, S], F32, name="neg_s", bufs=6)
            nc.vector.tensor_scalar(
                out=tiles["neg_s", i][:], in0=tiles["score_bank", i][:], scalar1=-SCALE, scalar2=None,
                op0=ALU.mult, op1=ALU.min, accum_out=tiles["neg_max"][:, i : i + 1],
            )

        def exponentials(j):
            tiles = live[j]
            tiles["e_sb"] = flow.tile([P, PAIR * S], BF16, name="e_sb")
            if j % 2 == 0:
                tiles["row_sum"] = flow.tile([P, 2, PAIR], F32, name="row_sum")
            else:
                tiles["row_sum"] = live[j - 1]["row_sum"]
            for i in range(PAIR):
                nc.scalar.activation(
                    out=tiles["e_sb"][:, i * S : (i + 1) * S], in_=tiles["neg_s", i][:], func=ACT.Exp,
                    scale=-1.0, bias=tiles["neg_max"][:, i : i + 1], accum_out=tiles["row_sum"][:, j % 2, i : i + 1],
                )

        def transpose_e(j):
            live[j]["et_bank"] = transpose_pairs(live[j]["e_sb"], S // 2, 0, 0, et_ps, "et")

        def copy_e(j):
            if j % 2 == 0:
                live[j]["e_grouped"] = flow.tile([P, 2 * PAIR * P * 2], F32, name="e_grouped", align_bytes=64)
            copy_pairs(live[j]["et_bank"], rows_of(live[j - j % 2]["e_grouped"], 0, j % 2))

        def quantise_e(j):
            tiles = live[j]
            tiles["e_codes"] = flow.tile([P, 2 * PAIR * P], U32, name="e_codes", align_bytes=64)
            tiles["e_scales"] = flow.tile([P, 2 * PAIR * P], U8, name="e_scales", align_bytes=64)
            nc.vector.quantize_mx(
                out=tiles["e_codes"][:].bitcast(FP8X4), scales=tiles["e_scales"][:], in_=tiles["e_grouped"][:].bitcast(BF16)
            )

        def e_times_v(j):
            b, a, h = steps[j]
            tiles = live[j]
            both = live[j - j % 2]
            if j == n_steps - 1:
                bank = v_ps.tile([P, PAIR, DH], F32, name="o_bank", tag="v_bank")
            else:
                bank = o_ps.tile([P, PAIR, DH], F32, name="o_bank", tag="o_bank")
            for i in range(PAIR):
                rows = slice((PAIR * (j % 2) + i) * P, (PAIR * (j % 2) + i + 1) * P)
                nc.tensor.matmul_mx(
                    out=bank[:, i, :],
                    lhsT=both["e_codes"][:, rows].bitcast(FP8X4),
                    lhsT_scale=both["e_scales"][:, rows],
                    rhs=batch[b]["v_codes"][:, h * DH : (h + 1) * DH].bitcast(FP8X4),
                    rhs_scale=batch[b]["v_scales"][:, h * DH : (h + 1) * DH],
                    start=True,
                    stop=True,
                )
            tiles["o_bank"] = bank

        def invert_row_sums(j):
            tiles = live[j]
            tiles["inv_sum"] = flow.tile([P, 2, PAIR], F32, name="inv_sum")
            nc.vector.reciprocal(out=tiles["inv_sum"][:], in_=tiles["row_sum"][:])

        def apply_mask(j):
            b, a, h = steps[j]
            first = ((H * b + h) % B) * TILES
            two_batches = mask01[:, first : first + 2 * TILES].rearrange("p (n t) -> p n t", n=2)
            row_scale = flow.tile([P, 2, PAIR], F32, name="row_scale")
            nc.vector.tensor_tensor(
                out=row_scale[:], in0=live[j]["inv_sum"][:], in1=two_batches[:, :, PAIR * a : PAIR * (a + 1)], op=ALU.mult
            )
            live[j]["row_scale"] = row_scale
            live[j + 1]["row_scale"] = row_scale

        def add_residual(j):
            b, a, h = steps[j]
            tiles = live[j]
            if h == 0:
                y_of[b, a] = {
                    "y": flow.tile([P, PAIR, D], F32, name="y"),
                    "stats": flow.tile([P, PAIR, 6], F32, name="stats"),
                }
            for i in range(PAIR):
                nc.vector.scalar_tensor_tensor(
                    out=y_of[b, a]["y"][:, i, h * DH : (h + 1) * DH], in0=tiles["o_bank"][:, i, :],
                    scalar=tiles["row_scale"][:, j % 2, i : i + 1], in1=x_sb[:, b, PAIR * a + i, h * DH : (h + 1) * DH],
                    op0=ALU.mult, op1=ALU.add,
                )

        def statistics(b, a, i):
            nc.vector.bn_stats(out=y_of[b, a]["stats"][:, i, :], in_=y_of[b, a]["y"][:, i, :])

        def aggregate(b, a):
            mean_var = flow.tile([P, PAIR, 2], F32, name="mean_var")
            for i in range(PAIR):
                nc.vector.bn_aggr(out=mean_var[:, i, :], in_=y_of[b, a]["stats"][:, i, :])
            y_of[b, a]["mean_var"] = mean_var

        def store(b, a, i):
            first = (a * PAIR + i) * P
            nc.sync.dma_start(out=out[b, first : first + P, :], in_=y_of[b, a]["y"][:, i, :])

        def layer_norm(b, a):
            y = y_of[b, a]["y"]
            mean_var = y_of[b, a]["mean_var"]
            inv_std = flow.tile([P, PAIR], F32, name="inv_std")
            var_eps = flow.tile([P, PAIR], F32, name="var_eps")
            nc.gpsimd.tensor_scalar(
                out=var_eps[:], in0=mean_var[:, :, 1], scalar1=LN_EPS, scalar2=1.0, op0=ALU.add, op1=ALU.mult
            )
            neg_mean = flow.tile([P, PAIR], F32, name="neg_mean")
            nc.gpsimd.tensor_scalar(
                out=neg_mean[:], in0=mean_var[:, :, 0], scalar1=-1.0, scalar2=0.0, op0=ALU.mult, op1=ALU.add
            )
            nc.gpsimd.tensor_tensor(out=inv_std[:], in0=var_eps[:], in1=neg_half[:], op=ALU.pow)
            for i in range(PAIR):
                nc.gpsimd.tensor_scalar(
                    out=y[:, i, :], in0=y[:, i, :], scalar1=neg_mean[:, i : i + 1],
                    scalar2=inv_std[:, i : i + 1], op0=ALU.add, op1=ALU.mult,
                )
            pieces = [(i, slice(first, first + LN_PIECE)) for i in range(PAIR) for first in range(0, D, LN_PIECE)]
            for i, cols in pieces:
                nc.gpsimd.tensor_tensor(out=y[:, i, cols], in0=y[:, i, cols], in1=gamma_bc[:, cols], op=ALU.mult)
            for i, cols in pieces:
                nc.gpsimd.tensor_tensor(out=y[:, i, cols], in0=y[:, i, cols], in1=beta_bc[:, cols], op=ALU.add)
            for i in range(PAIR):
                store(b, a, i)

        def centre(b, a):
            y = y_of[b, a]["y"]
            for i in range(PAIR):
                nc.vector.scalar_tensor_tensor(
                    out=y[:, i, :], in0=y[:, i, :], scalar=y_of[b, a]["mean_var"][:, i, 0:1], in1=gamma_bc[:],
                    op0=ALU.subtract, op1=ALU.mult,
                )

        def deviation(b, a):
            std = flow.tile([P, PAIR], F32, name="std")
            nc.scalar.activation(out=std[:], in_=y_of[b, a]["mean_var"][:, :, 1], func=ACT.Sqrt, bias=eps_col[:])
            y_of[b, a]["std"] = std

        def rescale(b, a):
            y = y_of[b, a]["y"]
            inv_std = flow.tile([P, PAIR], F32, name="inv_std")
            nc.vector.reciprocal(out=inv_std[:], in_=y_of[b, a]["std"][:])
            for i in range(PAIR):
                nc.vector.scalar_tensor_tensor(
                    out=y[:, i, :], in0=y[:, i, :], scalar=inv_std[:, i : i + 1], in1=beta_bc[:],
                    op0=ALU.mult, op1=ALU.add,
                )
                store(b, a, i)

        def is_step(j):
            return 0 <= j < n_steps

        def completes_rows(j):
            return is_step(j) and steps[j][2] == H - 1

        with tc.manual_schedule():
            head()
            tail = n_steps - H + ATTEND_LAG
            last, before_last = (B - 1, HALVES - 1), (B - 1, HALVES - 2)
            for j in range(n_steps + ATTEND_LAG - 1):
                b = j // SLOTS
                slot = j % SLOTS
                if slot == 0 and b + 3 < B:
                    load_keys(b + 3)
                if slot == 0 and b + 2 < B:
                    load_heads(b + 2)

                if is_step(j - EXP_LAG):
                    exponentials(j - EXP_LAG)
                if is_step(j - COPY_LAG):
                    copy_e(j - COPY_LAG)
                if slot < 4 and b + 2 < B:
                    keys_bank(b + 2, slot // 2, slot % 2)
                if slot >= 4 and b + 1 < B:
                    heads_ps, heads = heads_bank(b + 1, slot - 4)
                    if slot in SCALAR_HEADS:
                        nc.scalar.copy(out=heads, in_=heads_ps)
                if slot == 6 and b + 1 < B:
                    values_bank(b + 1, 0)
                if slot == 0 and b < B:
                    values_bank(b, 1)

                if is_step(j - ATTEND_LAG) and (j - ATTEND_LAG) % 2 == 0:
                    apply_mask(j - ATTEND_LAG)
                    quantise_e(j - ATTEND_LAG)
                if j == n_steps + ATTEND_LAG - 2:
                    centre(*before_last)
                if slot == 3 and b < B:
                    quantise_values(b)
                if slot == 7 and b + 2 < B:
                    quantise_keys(b + 2)
                if is_step(j - ATTEND_LAG):
                    e_times_v(j - ATTEND_LAG)
                if b + 1 < B:
                    project_values(b + 1, slot)

                for i in range(PAIR):
                    if is_step(j) and j > 0:
                        row_max(j, i)
                    if is_step(j + 1) and j > 0:
                        scores(j + 1, i)
                    if i == 0 and is_step(j + 1 - ATTEND_LAG) and (j + 1 - ATTEND_LAG) % 2 == 0:
                        invert_row_sums(j + 1 - ATTEND_LAG)
                if is_step(j - EXP_LAG):
                    transpose_e(j - EXP_LAG)

                if slot >= 4 and slot not in SCALAR_HEADS and b + 1 < B:
                    nc.vector.tensor_copy(out=heads, in_=heads_ps)
                if 0 < j < B:
                    row_mask(j)
                if 0 < j <= B:
                    compare_sums(j - 1)

                for i in range(PAIR):
                    if completes_rows(j - STATS_LAG - i) and j < tail:
                        statistics(steps[j - STATS_LAG - i][0], steps[j - STATS_LAG - i][1], i)
                if j == tail:
                    for i in range(PAIR):
                        statistics(*before_last, i)
                if is_step(j - ATTEND_LAG):
                    add_residual(j - ATTEND_LAG)
                if completes_rows(j - STATS_LAG - (PAIR - 1)) and j < tail:
                    rows = (steps[j - STATS_LAG - (PAIR - 1)][0], steps[j - STATS_LAG - (PAIR - 1)][1])
                    aggregate(*rows)
                    layer_norm(*rows)
                if j == tail:
                    aggregate(*before_last)
                if j == tail + 1:
                    deviation(*before_last)
            e_times_v(n_steps - 1)
            add_residual(n_steps - 1)
            for i in range(PAIR):
                statistics(*last, i)
            rescale(*before_last)
            aggregate(*last)
            deviation(*last)
            centre(*last)
            rescale(*last)
